import numpy as np
import ml_dtypes


def mxq(x, axis, fmt="e4m3"):
    dtype, down = {"e4m3": (ml_dtypes.float8_e4m3fn, 7), "e5m2": (ml_dtypes.float8_e5m2, 14)}[fmt]
    v = np.moveaxis(np.asarray(x, np.float32).astype(ml_dtypes.bfloat16).astype(np.float64), axis, -1)
    blocks = v.reshape(v.shape[:-1] + (-1, 32))
    amax = np.abs(blocks).max(-1, keepdims=True)
    byte = np.maximum(np.where(amax > 0, np.frexp(amax)[1] - 1 + 127, 0) - down, 1)
    scale = np.exp2(byte - 127.0)
    codes = (blocks / scale).astype(np.float32).astype(dtype).astype(np.float64)
    return np.moveaxis((codes * scale).reshape(v.shape), -1, axis)


WIDE = False


def mx_kscale(k):
    if not WIDE:
        return np.ones(k)
    levels = np.array([10, -10, 5, -5, 0])
    a = np.random.permutation(np.resize(levels, k // 512 * 4)).reshape(k // 512, 4)
    idx = np.arange(k)
    return np.exp2(a[idx // 512, idx % 128 // 32])


BF16 = ml_dtypes.bfloat16


def bf(x):
    return np.asarray(x, np.float32).astype(BF16)


def f64(x):
    return np.asarray(x).astype(np.float64)


B, L, S, H, D = 2, 4096, 512, 2, 256


def setup_inputs():
    t = mx_kscale(S)
    return {"queries": bf(np.random.standard_normal((B, L, H, D)) * 1.5),
            "keys": bf(np.random.standard_normal((B, S, H, D))),
            "values": bf(np.random.standard_normal((B, S, H, D)) * 2.0 * (np.mean(t) / t)[None, :, None, None]),
            "tau": bf(np.random.random(B) + 0.5),
            "delta": bf(np.random.standard_normal((B, S)) * 0.5 * np.sqrt(D) + np.log(t)[None, :] * np.sqrt(D))}


def reference(queries, keys, values, tau, delta):
    head_dim = queries.shape[-1]
    scale = 1.0 / np.sqrt(head_dim)
    scores = f64(queries).transpose(0, 2, 1, 3) @ f64(keys).transpose(0, 2, 3, 1)
    scores = scores * f64(tau)[:, None, None, None] + f64(delta)[:, None, None, :]
    z = scale * scores
    e = np.exp(z - z.max(-1, keepdims=True))
    v = mxq(f64(values), 1, "e4m3").transpose(0, 2, 1, 3)
    out = (mxq(e, 3, "e4m3") @ v) / e.sum(-1, keepdims=True)
    return out.transpose(0, 2, 1, 3)

@@ -1,0 +1,229 @@
+from contextlib import ExitStack
+
+import concourse.bass as bass
+import concourse.masks as masks
+import concourse.mybir as mybir
+import concourse.tile as tile
+
+F32 = mybir.dt.float32
+BF16 = mybir.dt.bfloat16
+U32 = mybir.dt.uint32
+U8 = mybir.dt.uint8
+FP8X4 = mybir.dt.float8_e4m3fn_x4
+ALU = mybir.AluOpType
+ACT = mybir.ActivationFunctionType
+AX = mybir.AxisListType
+
+B, L, S, H, D = 2, 4096, 512, 2, 256
+P = 128
+J = L // P
+PAIRS = B * J
+CH = 4
+QCH = 8
+FLOPS = 2 * 2 * B * H * L * S * D
+MANUAL = True
+
+
+def tile_dsattention_t_kernel(tc, queries, keys, values, tau, delta, out):
+    nc = tc.nc
+    with ExitStack() as ctx:
+        const = ctx.enter_context(tc.tile_pool(name="const", bufs=1))
+        work = ctx.enter_context(tc.tile_pool(name="work", bufs=3))
+        psum = ctx.enter_context(tc.psum_pool(name="psum", bufs=1))
+        if MANUAL:
+            ctx.enter_context(tc.manual_schedule())
+
+        k_raw = [const.tile([P, 4 * H * D], BF16, name="k_raw%d" % b) for b in range(B)]
+        v_raw = [const.tile([P, 4 * H * D], BF16, name="v_raw%d" % b) for b in range(B)]
+        q_sb = [const.tile([P, J * H * D], BF16, name="q_sb%d" % b) for b in range(B)]
+        tau_bf = const.tile([P, B], BF16, name="tau_bf")
+        delta_bf = const.tile([P, B * S], BF16, name="delta_bf")
+
+        def load_kv(dst, src, b):
+            nc.sync.dma_start(
+                out=dst[b][:].rearrange("p (t c) -> p t c", t=4),
+                in_=src[b].rearrange("(t p) h d -> p t (h d)", p=P),
+            )
+
+        def load_q(b, c):
+            nc.sync.dma_start(
+                out=q_sb[b][:].rearrange("p (j c) -> p j c", j=J)[:, c * QCH:(c + 1) * QCH, :],
+                in_=queries[b].rearrange("(p j) h d -> p j (h d)", j=J)[:, c * QCH:(c + 1) * QCH, :],
+            )
+
+        load_kv(k_raw, keys, 0)
+        load_q(0, 0)
+        nc.sync.dma_start(out=tau_bf[:], in_=tau.partition_broadcast(P))
+        nc.sync.dma_start(out=delta_bf[:], in_=delta.rearrange("b s -> (b s)").partition_broadcast(P))
+        load_kv(v_raw, values, 0)
+        load_kv(k_raw, keys, 1)
+        load_kv(v_raw, values, 1)
+        for c in range(1, J // QCH):
+            load_q(0, c)
+        for c in range(J // QCH):
+            load_q(1, c)
+
+        ident_f = const.tile([P, P], F32, name="ident_f")
+        masks.make_identity(nc, ident_f[:])
+        ident_b = const.tile([P, P], BF16, name="ident_b")
+        masks.make_identity(nc, ident_b[:])
+        ntau = const.tile([P, B], F32, name="ntau")
+        nc.vector.tensor_scalar_mul(out=ntau[:], in0=tau_bf[:], scalar1=-1.0 / 16.0)
+        ndelta = const.tile([P, B * S], F32, name="ndelta")
+        nc.vector.tensor_scalar_mul(out=ndelta[:], in0=delta_bf[:], scalar1=-1.0 / 16.0)
+
+        k_t = [[const.tile([P, S], F32, name="k_t%d%d" % (b, h)) for h in range(H)] for b in range(B)]
+        v_codes = [const.tile([P, H * D], U32, name="v_codes%d" % b, align_bytes=64) for b in range(B)]
+        v_scales = [const.tile([P, H * D], U8, name="v_scales%d" % b, align_bytes=64) for b in range(B)]
+
+        def prepare_keys(b, h):
+            words = k_raw[b][:].bitcast(F32)
+            kt_ps = psum.tile([P, S], F32, name="kt_ps", tag="sc", bufs=3)
+            for t in range(4):
+                c0 = t * (H * D // 2) + h * (D // 2)
+                nc.tensor.transpose(kt_ps[:, t * P:(t + 1) * P], words[:, c0:c0 + P], ident_f[:])
+            if h == 0:
+                nc.scalar.copy(out=k_t[b][h][:], in_=kt_ps[:])
+            else:
+                nc.vector.tensor_copy(out=k_t[b][h][:], in_=kt_ps[:])
+
+        def prepare_values(b):
+            v_grp = work.tile([P, 4 * H * D], BF16, name="v_grp", tag="v_grp", bufs=2, align_bytes=64)
+            nc.vector.tensor_copy(
+                out=v_grp[:].rearrange("p (c t) -> p c t", t=4),
+                in_=v_raw[b][:].rearrange("p (t c) -> p c t", t=4),
+            )
+            return v_grp
+
+        def quantise_values(b, v_grp):
+            nc.vector.quantize_mx(out=v_codes[b][:].bitcast(FP8X4), scales=v_scales[b][:], in_=v_grp[:])
+
+        for b in range(B):
+            for h in range(H):
+                prepare_keys(b, h)
+        grp = [prepare_values(b) for b in range(B)]
+        for b in range(B):
+            quantise_values(b, grp[b])
+
+        qt_ps, q_t, sc, nz, mn, rs, e_sb, et, g, codes, scl, rinv, pv, o_sb = (
+            {}, {}, {}, {}, {}, {}, {}, {}, {}, {}, {}, {}, {}, {})
+
+        def ok(n):
+            return 0 <= n < PAIRS
+
+        def st_qt(n):
+            b, j = n // J, n % J
+            words = q_sb[b][:].bitcast(F32)
+            qt_ps[n] = psum.tile([P, H * P], F32, name="qt_ps", tag="qt", bufs=1)
+            for h in range(H):
+                c0 = j * (H * D // 2) + h * (D // 2)
+                nc.tensor.transpose(qt_ps[n][:, h * P:(h + 1) * P], words[:, c0:c0 + P], ident_f[:])
+
+        def st_w7(n):
+            q_t[n] = work.tile([P, H * P], F32, name="q_t", tag="q_t", bufs=3)
+            nc.scalar.copy(out=q_t[n][:], in_=qt_ps[n][:])
+
+        def st_qk(n, h):
+            b = n // J
+            sc[n, h] = psum.tile([P, S], F32, name="sc", tag="sc", bufs=3)
+            qv = q_t[n][:].bitcast(BF16).rearrange("p (h l e) -> p h l e", h=H, e=2)
+            kv = k_t[b][h][:].bitcast(BF16).rearrange("p (s e) -> p s e", e=2)
+            for e in range(2):
+                nc.tensor.matmul(sc[n, h][:], lhsT=qv[:, h, :, e], rhs=kv[:, :, e], start=(e == 0), stop=(e == 1))
+
+        def st_w12(n, h):
+            b = n // J
+            nz[n, h] = work.tile([P, S], F32, name="nz", tag="nz", bufs=3)
+            nc.vector.scalar_tensor_tensor(
+                out=nz[n, h][:], in0=sc[n, h][:], scalar=ntau[:, b:b + 1],
+                in1=ndelta[:, b * S:(b + 1) * S], op0=ALU.mult, op1=ALU.add)
+            if h == 0:
+                mn[n] = work.tile([P, H], F32, name="mn", tag="mn", bufs=4)
+            nc.vector.tensor_reduce(out=mn[n][:, h:h + 1], in_=nz[n, h][:], axis=AX.X, op=ALU.min)
+
+        def st_w3(n, h):
+            if h == 0:
+                rs[n] = work.tile([P, H], F32, name="rs", tag="rs", bufs=6)
+            e_sb[n, h] = work.tile([P, S], BF16, name="e_sb", tag="e_sb", bufs=4)
+            nc.scalar.activation(
+                out=e_sb[n, h][:], in_=nz[n, h][:], func=ACT.Exp, bias=mn[n][:, h:h + 1], scale=-1.0,
+                accum_out=rs[n][:, h:h + 1])
+
+        def st_et(n, h):
+            et[n, h] = psum.tile([P, S], BF16, name="et", tag="et", bufs=2)
+            for t in range(4):
+                nc.tensor.transpose(et[n, h][:, t * P:(t + 1) * P], e_sb[n, h][:, t * P:(t + 1) * P], ident_b[:])
+
+        def st_w4(n, h):
+            if h == 0:
+                g[n] = work.tile([P, H * S], BF16, name="g", tag="g", bufs=3, align_bytes=64)
+            nc.scalar.copy(
+                out=g[n][:, h * S:(h + 1) * S].rearrange("p (l t) -> p l t", t=4),
+                in_=et[n, h][:].rearrange("p (t l) -> p l t", t=4))
+
+        def st_w5(n):
+            codes[n] = work.tile([P, H * P], U32, name="codes", tag="codes", bufs=3, align_bytes=64)
+            scl[n] = work.tile([P, H * P], U8, name="scl", tag="scl", bufs=3, align_bytes=64)
+            nc.vector.quantize_mx(out=codes[n][:].bitcast(FP8X4), scales=scl[n][:], in_=g[n][:])
+            rinv[n] = work.tile([P, H], F32, name="rinv", tag="rinv", bufs=4)
+            nc.vector.reciprocal(out=rinv[n][:], in_=rs[n][:])
+
+        def st_pv(n, h):
+            b = n // J
+            pv[n, h] = psum.tile([P, D], F32, name="pv", tag="pv", bufs=2)
+            nc.tensor.matmul_mx(
+                out=pv[n, h][:],
+                lhsT=codes[n][:, h * P:(h + 1) * P].bitcast(FP8X4),
+                lhsT_scale=scl[n][:, h * P:(h + 1) * P],
+                rhs=v_codes[b][:, h * D:(h + 1) * D].bitcast(FP8X4),
+                rhs_scale=v_scales[b][:, h * D:(h + 1) * D],
+                start=True, stop=True)
+
+        def st_w6(n, h):
+            c = n // CH
+            if n % CH == 0 and h == 0:
+                o_sb[c] = work.tile([P, CH * H * D], F32, name="o_sb", tag="o_sb", bufs=3)
+            c0 = ((n % CH) * H + h) * D
+            dst = o_sb[c][:, c0:c0 + D]
+            if h == 0:
+                nc.vector.tensor_scalar_mul(out=dst, in0=pv[n, h][:], scalar1=rinv[n][:, h:h + 1])
+            else:
+                nc.scalar.activation(out=dst, in_=pv[n, h][:], func=ACT.Copy, scale=rinv[n][:, h:h + 1])
+                if n % CH == CH - 1:
+                    b, j = n // J, n % J
+                    nc.sync.dma_start(
+                        out=out[b].rearrange("(p j) h d -> p j (h d)", j=J)[:, j - CH + 1:j + 1, :],
+                        in_=o_sb[c][:].rearrange("p (j c) -> p j c", j=CH))
+
+        for n in range(-3, PAIRS + 4):
+            if ok(n - 1):
+                st_w3(n - 1, 1)
+            if ok(n + 1):
+                st_qk(n + 1, 0)
+            if ok(n):
+                st_w12(n, 0)
+            if ok(n + 1):
+                st_qk(n + 1, 1)
+            if ok(n + 2):
+                st_w7(n + 2)
+            if ok(n - 3):
+                st_w6(n - 3, 1)
+            if ok(n - 1):
+                st_et(n - 1, 0)
+                st_et(n - 1, 1)
+            if ok(n + 3):
+                st_qt(n + 3)
+            if ok(n - 2):
+                st_w5(n - 2)
+            if ok(n):
+                st_w3(n, 0)
+            if ok(n - 2):
+                st_pv(n - 2, 0)
+                st_pv(n - 2, 1)
+            if ok(n):
+                st_w12(n, 1)
+            if ok(n - 1):
+                st_w4(n - 1, 0)
+                st_w4(n - 1, 1)
+            if ok(n - 2):
+                st_w6(n - 2, 0)

@@ -18,7 +18,7 @@ B, L, S, H, D = 2, 4096, 512, 2, 256
 P = 128
 J = L // P
 PAIRS = B * J
-CH = 4
+CH = 2
 QCH = 8
 FLOPS = 2 * 2 * B * H * L * S * D
 MANUAL = True
@@ -45,65 +45,62 @@ def tile_dsattention_t_kernel(tc, queries, keys, values, tau, delta, out):
                 in_=src[b].rearrange("(t p) h d -> p t (h d)", p=P),
             )
 
-        def load_q(b, c):
+        def load_q(b, j0, j1):
             nc.sync.dma_start(
-                out=q_sb[b][:].rearrange("p (j c) -> p j c", j=J)[:, c * QCH:(c + 1) * QCH, :],
-                in_=queries[b].rearrange("(p j) h d -> p j (h d)", j=J)[:, c * QCH:(c + 1) * QCH, :],
+                out=q_sb[b][:].rearrange("p (j c) -> p j c", j=J)[:, j0:j1, :],
+                in_=queries[b].rearrange("(p j) h d -> p j (h d)", j=J)[:, j0:j1, :],
             )
 
         load_kv(k_raw, keys, 0)
-        load_q(0, 0)
+        load_q(0, 0, 2)
         nc.sync.dma_start(out=tau_bf[:], in_=tau.partition_broadcast(P))
         nc.sync.dma_start(out=delta_bf[:], in_=delta.rearrange("b s -> (b s)").partition_broadcast(P))
+        load_q(0, 2, QCH)
         load_kv(v_raw, values, 0)
         load_kv(k_raw, keys, 1)
         load_kv(v_raw, values, 1)
         for c in range(1, J // QCH):
-            load_q(0, c)
+            load_q(0, c * QCH, (c + 1) * QCH)
         for c in range(J // QCH):
-            load_q(1, c)
+            load_q(1, c * QCH, (c + 1) * QCH)
 
         ident_f = const.tile([P, P], F32, name="ident_f")
         masks.make_identity(nc, ident_f[:])
         ident_b = const.tile([P, P], BF16, name="ident_b")
         masks.make_identity(nc, ident_b[:])
         ntau = const.tile([P, B], F32, name="ntau")
-        nc.vector.tensor_scalar_mul(out=ntau[:], in0=tau_bf[:], scalar1=-1.0 / 16.0)
+        nc.gpsimd.tensor_scalar(out=ntau[:], in0=tau_bf[:], scalar1=-1.0 / 16.0, scalar2=0.0, op0=ALU.mult, op1=ALU.add)
         ndelta = const.tile([P, B * S], F32, name="ndelta")
-        nc.vector.tensor_scalar_mul(out=ndelta[:], in0=delta_bf[:], scalar1=-1.0 / 16.0)
+        nc.gpsimd.tensor_scalar(out=ndelta[:], in0=delta_bf[:], scalar1=-1.0 / 16.0, scalar2=0.0, op0=ALU.mult, op1=ALU.add)
 
         k_t = [[const.tile([P, S], F32, name="k_t%d%d" % (b, h)) for h in range(H)] for b in range(B)]
         v_codes = [const.tile([P, H * D], U32, name="v_codes%d" % b, align_bytes=64) for b in range(B)]
         v_scales = [const.tile([P, H * D], U8, name="v_scales%d" % b, align_bytes=64) for b in range(B)]
 
-        def prepare_keys(b, h):
+        def prepare_keys(b, h, tag, bufs):
             words = k_raw[b][:].bitcast(F32)
-            kt_ps = psum.tile([P, S], F32, name="kt_ps", tag="sc", bufs=3)
+            kt_ps = psum.tile([P, S], F32, name="kt_ps", tag=tag, bufs=bufs)
             for t in range(4):
                 c0 = t * (H * D // 2) + h * (D // 2)
                 nc.tensor.transpose(kt_ps[:, t * P:(t + 1) * P], words[:, c0:c0 + P], ident_f[:])
-            if h == 0:
-                nc.scalar.copy(out=k_t[b][h][:], in_=kt_ps[:])
-            else:
-                nc.vector.tensor_copy(out=k_t[b][h][:], in_=kt_ps[:])
+            return kt_ps
 
-        def prepare_values(b):
-            v_grp = work.tile([P, 4 * H * D], BF16, name="v_grp", tag="v_grp", bufs=2, align_bytes=64)
-            nc.vector.tensor_copy(
+        def regroup_values(b):
+            v_grp = const.tile([P, 4 * H * D], BF16, name="v_grp%d" % b, align_bytes=64)
+            nc.gpsimd.tensor_scalar(
                 out=v_grp[:].rearrange("p (c t) -> p c t", t=4),
-                in_=v_raw[b][:].rearrange("p (t c) -> p c t", t=4),
-            )
+                in0=v_raw[b][:].rearrange("p (t c) -> p c t", t=4),
+                scalar1=1.0, scalar2=0.0, op0=ALU.mult, op1=ALU.add)
             return v_grp
 
-        def quantise_values(b, v_grp):
-            nc.vector.quantize_mx(out=v_codes[b][:].bitcast(FP8X4), scales=v_scales[b][:], in_=v_grp[:])
+        def quantise_values(b):
+            nc.vector.quantize_mx(out=v_codes[b][:].bitcast(FP8X4), scales=v_scales[b][:], in_=grp[b][:])
 
-        for b in range(B):
-            for h in range(H):
-                prepare_keys(b, h)
-        grp = [prepare_values(b) for b in range(B)]
-        for b in range(B):
-            quantise_values(b, grp[b])
+        kt0 = prepare_keys(0, 0, "sc", 3)
+        nc.scalar.copy(out=k_t[0][0][:], in_=kt0[:])
+        kt1 = prepare_keys(0, 1, "sc", 3)
+        nc.vector.tensor_copy(out=k_t[0][1][:], in_=kt1[:])
+        grp = [regroup_values(b) for b in range(B)]
 
         qt_ps, q_t, sc, nz, mn, rs, e_sb, et, g, codes, scl, rinv, pv, o_sb = (
             {}, {}, {}, {}, {}, {}, {}, {}, {}, {}, {}, {}, {}, {})
@@ -131,22 +128,23 @@ def tile_dsattention_t_kernel(tc, queries, keys, values, tau, delta, out):
             for e in range(2):
                 nc.tensor.matmul(sc[n, h][:], lhsT=qv[:, h, :, e], rhs=kv[:, :, e], start=(e == 0), stop=(e == 1))
 
-        def st_w12(n, h):
+        def st_w1(n, h):
             b = n // J
-            nz[n, h] = work.tile([P, S], F32, name="nz", tag="nz", bufs=3)
+            nz[n, h] = work.tile([P, S], F32, name="nz", tag="nz", bufs=6)
             nc.vector.scalar_tensor_tensor(
                 out=nz[n, h][:], in0=sc[n, h][:], scalar=ntau[:, b:b + 1],
                 in1=ndelta[:, b * S:(b + 1) * S], op0=ALU.mult, op1=ALU.add)
-            if h == 0:
-                mn[n] = work.tile([P, H], F32, name="mn", tag="mn", bufs=4)
-            nc.vector.tensor_reduce(out=mn[n][:, h:h + 1], in_=nz[n, h][:], axis=AX.X, op=ALU.min)
+
+        def st_w2(n, h):
+            mn[n, h] = work.tile([P, 1], F32, name="mn", tag="mn", bufs=8)
+            nc.vector.tensor_reduce(out=mn[n, h][:], in_=nz[n, h][:], axis=AX.X, op=ALU.min)
 
         def st_w3(n, h):
             if h == 0:
                 rs[n] = work.tile([P, H], F32, name="rs", tag="rs", bufs=6)
-            e_sb[n, h] = work.tile([P, S], BF16, name="e_sb", tag="e_sb", bufs=4)
+            e_sb[n, h] = work.tile([P, S], BF16, name="e_sb", tag="e_sb", bufs=5)
             nc.scalar.activation(
-                out=e_sb[n, h][:], in_=nz[n, h][:], func=ACT.Exp, bias=mn[n][:, h:h + 1], scale=-1.0,
+                out=e_sb[n, h][:], in_=nz[n, h][:], func=ACT.Exp, bias=mn[n, h][:], scale=-1.0,
                 accum_out=rs[n][:, h:h + 1])
 
         def st_et(n, h):
@@ -195,35 +193,46 @@ def tile_dsattention_t_kernel(tc, queries, keys, values, tau, delta, out):
                         out=out[b].rearrange("(p j) h d -> p j (h d)", j=J)[:, j - CH + 1:j + 1, :],
                         in_=o_sb[c][:].rearrange("p (j c) -> p j c", j=CH))
 
-        for n in range(-3, PAIRS + 4):
-            if ok(n - 1):
-                st_w3(n - 1, 1)
-            if ok(n + 1):
-                st_qk(n + 1, 0)
-            if ok(n):
-                st_w12(n, 0)
-            if ok(n + 1):
-                st_qk(n + 1, 1)
+        for n in range(-3, PAIRS + 5):
+            if ok(n - 4):
+                st_w6(n - 4, 1)
             if ok(n + 2):
                 st_w7(n + 2)
             if ok(n - 3):
-                st_w6(n - 3, 1)
-            if ok(n - 1):
-                st_et(n - 1, 0)
-                st_et(n - 1, 1)
+                st_w5(n - 3)
+            elif n in (0, 1):
+                quantise_values(n)
+            if ok(n - 2):
+                st_et(n - 2, 0)
+                st_et(n - 2, 1)
+            if ok(n + 1):
+                st_qk(n + 1, 1)
+            if ok(n - 3):
+                st_pv(n - 3, 0)
+                st_pv(n - 3, 1)
+            elif n in (0, 1):
+                kt1 = prepare_keys(1, n, "pv", 2)
             if ok(n + 3):
                 st_qt(n + 3)
-            if ok(n - 2):
-                st_w5(n - 2)
             if ok(n):
-                st_w3(n, 0)
-            if ok(n - 2):
-                st_pv(n - 2, 0)
-                st_pv(n - 2, 1)
+                st_w1(n, 1)
+            if ok(n + 2):
+                st_qk(n + 2, 0)
             if ok(n):
-                st_w12(n, 1)
+                st_w2(n, 0)
+            if ok(n + 1):
+                st_w1(n + 1, 0)
+            if ok(n - 3):
+                st_w6(n - 3, 0)
+            if ok(n):
+                st_w2(n, 1)
             if ok(n - 1):
-                st_w4(n - 1, 0)
-                st_w4(n - 1, 1)
+                st_w3(n - 1, 0)
             if ok(n - 2):
-                st_w6(n - 2, 0)
+                st_w4(n - 2, 0)
+            elif n in (0, 1):
+                nc.scalar.copy(out=k_t[1][n][:], in_=kt1[:])
+            if ok(n - 1):
+                st_w3(n - 1, 1)
+            if ok(n - 2):
+                st_w4(n - 2, 1)

@@ -18,7 +18,7 @@ B, L, S, H, D = 2, 4096, 512, 2, 256
 P = 128
 J = L // P
 PAIRS = B * J
-CH = 2
+QUADS = PAIRS // 2
 QCH = 8
 FLOPS = 2 * 2 * B * H * L * S * D
 MANUAL = True
@@ -102,137 +102,171 @@ def tile_dsattention_t_kernel(tc, queries, keys, values, tau, delta, out):
         nc.vector.tensor_copy(out=k_t[0][1][:], in_=kt1[:])
         grp = [regroup_values(b) for b in range(B)]
 
-        qt_ps, q_t, sc, nz, mn, rs, e_sb, et, g, codes, scl, rinv, pv, o_sb = (
-            {}, {}, {}, {}, {}, {}, {}, {}, {}, {}, {}, {}, {}, {})
+        qt_ps, q_t, sc, nz, mn, rs, e_sb, et, et_sb, g, codes, scl, rinv, pv, o_sb = (
+            {}, {}, {}, {}, {}, {}, {}, {}, {}, {}, {}, {}, {}, {}, {})
 
-        def ok(n):
-            return 0 <= n < PAIRS
+        def ok(k):
+            return 0 <= k < QUADS
 
-        def st_qt(n):
-            b, j = n // J, n % J
-            words = q_sb[b][:].bitcast(F32)
-            qt_ps[n] = psum.tile([P, H * P], F32, name="qt_ps", tag="qt", bufs=1)
-            for h in range(H):
-                c0 = j * (H * D // 2) + h * (D // 2)
-                nc.tensor.transpose(qt_ps[n][:, h * P:(h + 1) * P], words[:, c0:c0 + P], ident_f[:])
+        def st_qt(k):
+            qt_ps[k] = psum.tile([P, 4 * P], F32, name="qt_ps", tag="qt", bufs=1)
+            for u in range(2):
+                m = 2 * k + u
+                words = q_sb[m // J][:].bitcast(F32)
+                for h in range(H):
+                    c0 = (m % J) * (H * D // 2) + h * (D // 2)
+                    i = u * H + h
+                    nc.tensor.transpose(qt_ps[k][:, i * P:(i + 1) * P], words[:, c0:c0 + P], ident_f[:])
 
-        def st_w7(n):
-            q_t[n] = work.tile([P, H * P], F32, name="q_t", tag="q_t", bufs=3)
-            nc.scalar.copy(out=q_t[n][:], in_=qt_ps[n][:])
+        def st_w7(k):
+            q_t[k] = work.tile([P, 4 * P], F32, name="q_t", tag="q_t", bufs=3)
+            nc.scalar.copy(out=q_t[k][:], in_=qt_ps[k][:])
 
-        def st_qk(n, h):
-            b = n // J
-            sc[n, h] = psum.tile([P, S], F32, name="sc", tag="sc", bufs=3)
-            qv = q_t[n][:].bitcast(BF16).rearrange("p (h l e) -> p h l e", h=H, e=2)
+        def st_qk(k, u, h):
+            m = 2 * k + u
+            b = m // J
+            sc[m, h] = psum.tile([P, S], F32, name="sc", tag="sc", bufs=3)
+            qv = q_t[k][:].bitcast(BF16).rearrange("p (i l e) -> p i l e", i=4, e=2)
             kv = k_t[b][h][:].bitcast(BF16).rearrange("p (s e) -> p s e", e=2)
             for e in range(2):
-                nc.tensor.matmul(sc[n, h][:], lhsT=qv[:, h, :, e], rhs=kv[:, :, e], start=(e == 0), stop=(e == 1))
+                nc.tensor.matmul(sc[m, h][:], lhsT=qv[:, u * H + h, :, e], rhs=kv[:, :, e], start=(e == 0), stop=(e == 1))
 
-        def st_w1(n, h):
-            b = n // J
-            nz[n, h] = work.tile([P, S], F32, name="nz", tag="nz", bufs=6)
+        def st_w1(k, u, h):
+            m = 2 * k + u
+            b = m // J
+            nz[m, h] = work.tile([P, S], F32, name="nz", tag="nz", bufs=6)
             nc.vector.scalar_tensor_tensor(
-                out=nz[n, h][:], in0=sc[n, h][:], scalar=ntau[:, b:b + 1],
+                out=nz[m, h][:], in0=sc[m, h][:], scalar=ntau[:, b:b + 1],
                 in1=ndelta[:, b * S:(b + 1) * S], op0=ALU.mult, op1=ALU.add)
 
-        def st_w2(n, h):
-            mn[n, h] = work.tile([P, 1], F32, name="mn", tag="mn", bufs=8)
-            nc.vector.tensor_reduce(out=mn[n, h][:], in_=nz[n, h][:], axis=AX.X, op=ALU.min)
+        def st_w2(k, u, h):
+            m = 2 * k + u
+            mn[m, h] = work.tile([P, 1], F32, name="mn", tag="mn", bufs=8)
+            nc.vector.tensor_reduce(out=mn[m, h][:], in_=nz[m, h][:], axis=AX.X, op=ALU.min)
 
-        def st_w3(n, h):
+        def st_w3(k, u, h):
+            m = 2 * k + u
+            if u == 0 and h == 0:
+                rs[k] = work.tile([P, 4], F32, name="rs", tag="rs", bufs=5)
             if h == 0:
-                rs[n] = work.tile([P, H], F32, name="rs", tag="rs", bufs=6)
-            e_sb[n, h] = work.tile([P, S], BF16, name="e_sb", tag="e_sb", bufs=5)
+                e_sb[m] = work.tile([P, H * S], BF16, name="e_sb", tag="e_sb", bufs=4)
+            i = u * H + h
             nc.scalar.activation(
-                out=e_sb[n, h][:], in_=nz[n, h][:], func=ACT.Exp, bias=mn[n, h][:], scale=-1.0,
-                accum_out=rs[n][:, h:h + 1])
+                out=e_sb[m][:, h * S:(h + 1) * S], in_=nz[m, h][:], func=ACT.Exp, bias=mn[m, h][:], scale=-1.0,
+                accum_out=rs[k][:, i:i + 1])
 
-        def st_et(n, h):
-            et[n, h] = psum.tile([P, S], BF16, name="et", tag="et", bufs=2)
-            for t in range(4):
-                nc.tensor.transpose(et[n, h][:, t * P:(t + 1) * P], e_sb[n, h][:, t * P:(t + 1) * P], ident_b[:])
+        def st_et(k, u):
+            m = 2 * k + u
+            et[m] = psum.tile([P, H * S], BF16, name="et", tag="et", bufs=2)
+            for i in range(8):
+                nc.tensor.transpose(et[m][:, i * P:(i + 1) * P], e_sb[m][:, i * P:(i + 1) * P], ident_b[:])
 
-        def st_w4(n, h):
-            if h == 0:
-                g[n] = work.tile([P, H * S], BF16, name="g", tag="g", bufs=3, align_bytes=64)
-            nc.scalar.copy(
-                out=g[n][:, h * S:(h + 1) * S].rearrange("p (l t) -> p l t", t=4),
-                in_=et[n, h][:].rearrange("p (t l) -> p l t", t=4))
+        def st_w4(k, u):
+            m = 2 * k + u
+            et_sb[m] = work.tile([P, H * S], BF16, name="et_sb", tag="et_sb", bufs=3)
+            nc.scalar.copy(out=et_sb[m][:], in_=et[m][:])
 
-        def st_w5(n):
-            codes[n] = work.tile([P, H * P], U32, name="codes", tag="codes", bufs=3, align_bytes=64)
-            scl[n] = work.tile([P, H * P], U8, name="scl", tag="scl", bufs=3, align_bytes=64)
-            nc.vector.quantize_mx(out=codes[n][:].bitcast(FP8X4), scales=scl[n][:], in_=g[n][:])
-            rinv[n] = work.tile([P, H], F32, name="rinv", tag="rinv", bufs=4)
-            nc.vector.reciprocal(out=rinv[n][:], in_=rs[n][:])
+        def st_rg(k, u):
+            m = 2 * k + u
+            if u == 0:
+                g[k] = work.tile([P, 2 * H * S], BF16, name="g", tag="g", bufs=1, align_bytes=64)
+            nc.gpsimd.tensor_scalar(
+                out=g[k][:, u * H * S:(u + 1) * H * S].rearrange("p (h l t) -> p h l t", h=H, t=4),
+                in0=et_sb[m][:].rearrange("p (h t l) -> p h l t", h=H, t=4),
+                scalar1=1.0, scalar2=0.0, op0=ALU.mult, op1=ALU.add)
 
-        def st_pv(n, h):
-            b = n // J
-            pv[n, h] = psum.tile([P, D], F32, name="pv", tag="pv", bufs=2)
-            nc.tensor.matmul_mx(
-                out=pv[n, h][:],
-                lhsT=codes[n][:, h * P:(h + 1) * P].bitcast(FP8X4),
-                lhsT_scale=scl[n][:, h * P:(h + 1) * P],
-                rhs=v_codes[b][:, h * D:(h + 1) * D].bitcast(FP8X4),
-                rhs_scale=v_scales[b][:, h * D:(h + 1) * D],
-                start=True, stop=True)
+        def st_w5(k):
+            codes[k] = work.tile([P, 4 * P], U32, name="codes", tag="codes", bufs=2, align_bytes=64)
+            scl[k] = work.tile([P, 4 * P], U8, name="scl", tag="scl", bufs=2, align_bytes=64)
+            nc.vector.quantize_mx(out=codes[k][:].bitcast(FP8X4), scales=scl[k][:], in_=g[k][:])
+            rinv[k] = work.tile([P, 4], F32, name="rinv", tag="rinv", bufs=3)
+            nc.vector.reciprocal(out=rinv[k][:], in_=rs[k][:])
 
-        def st_w6(n, h):
-            c = n // CH
-            if n % CH == 0 and h == 0:
-                o_sb[c] = work.tile([P, CH * H * D], F32, name="o_sb", tag="o_sb", bufs=3)
-            c0 = ((n % CH) * H + h) * D
-            dst = o_sb[c][:, c0:c0 + D]
-            if h == 0:
-                nc.vector.tensor_scalar_mul(out=dst, in0=pv[n, h][:], scalar1=rinv[n][:, h:h + 1])
-            else:
-                nc.scalar.activation(out=dst, in_=pv[n, h][:], func=ACT.Copy, scale=rinv[n][:, h:h + 1])
-                if n % CH == CH - 1:
-                    b, j = n // J, n % J
-                    nc.sync.dma_start(
-                        out=out[b].rearrange("(p j) h d -> p j (h d)", j=J)[:, j - CH + 1:j + 1, :],
-                        in_=o_sb[c][:].rearrange("p (j c) -> p j c", j=CH))
+        def st_pv(k, u):
+            m = 2 * k + u
+            b = m // J
+            pv[m] = psum.tile([P, H * D], F32, name="pv", tag="pv", bufs=2)
+            for h in range(H):
+                i = u * H + h
+                nc.tensor.matmul_mx(
+                    out=pv[m][:, h * D:(h + 1) * D],
+                    lhsT=codes[k][:, i * P:(i + 1) * P].bitcast(FP8X4),
+                    lhsT_scale=scl[k][:, i * P:(i + 1) * P],
+                    rhs=v_codes[b][:, h * D:(h + 1) * D].bitcast(FP8X4),
+                    rhs_scale=v_scales[b][:, h * D:(h + 1) * D],
+                    start=True, stop=True)
 
-        for n in range(-3, PAIRS + 5):
-            if ok(n - 4):
-                st_w6(n - 4, 1)
-            if ok(n + 2):
-                st_w7(n + 2)
-            if ok(n - 3):
-                st_w5(n - 3)
-            elif n in (0, 1):
-                quantise_values(n)
-            if ok(n - 2):
-                st_et(n - 2, 0)
-                st_et(n - 2, 1)
-            if ok(n + 1):
-                st_qk(n + 1, 1)
-            if ok(n - 3):
-                st_pv(n - 3, 0)
-                st_pv(n - 3, 1)
-            elif n in (0, 1):
-                kt1 = prepare_keys(1, n, "pv", 2)
-            if ok(n + 3):
-                st_qt(n + 3)
-            if ok(n):
-                st_w1(n, 1)
-            if ok(n + 2):
-                st_qk(n + 2, 0)
-            if ok(n):
-                st_w2(n, 0)
-            if ok(n + 1):
-                st_w1(n + 1, 0)
-            if ok(n - 3):
-                st_w6(n - 3, 0)
-            if ok(n):
-                st_w2(n, 1)
-            if ok(n - 1):
-                st_w3(n - 1, 0)
-            if ok(n - 2):
-                st_w4(n - 2, 0)
-            elif n in (0, 1):
-                nc.scalar.copy(out=k_t[1][n][:], in_=kt1[:])
-            if ok(n - 1):
-                st_w3(n - 1, 1)
-            if ok(n - 2):
-                st_w4(n - 2, 1)
+        def st_w6(k, u):
+            m = 2 * k + u
+            if u == 0:
+                o_sb[k] = work.tile([P, 4 * D], F32, name="o_sb", tag="o_sb", bufs=3)
+            for h in (1, 0):
+                i = u * H + h
+                nc.scalar.activation(
+                    out=o_sb[k][:, i * D:(i + 1) * D], in_=pv[m][:, h * D:(h + 1) * D], func=ACT.Copy,
+                    scale=rinv[k][:, i:i + 1])
+            if u == 1:
+                b, j = m // J, m % J
+                nc.sync.dma_start(
+                    out=out[b].rearrange("(p j) h d -> p j (h d)", j=J)[:, j - 1:j + 1, :],
+                    in_=o_sb[k][:].rearrange("p (j c) -> p j c", j=2))
+
+        for k in range(-2, QUADS + 4):
+            if ok(k + 1):
+                st_w7(k + 1)
+            if ok(k - 1):
+                st_w3(k - 1, 1, 0)
+                st_w3(k - 1, 1, 1)
+            if ok(k - 4):
+                st_w6(k - 4, 0)
+                st_w6(k - 4, 1)
+            if ok(k - 3):
+                st_w5(k - 3)
+            elif k in (0, 1):
+                quantise_values(k)
+            if ok(k - 2):
+                st_rg(k - 2, 0)
+                st_rg(k - 2, 1)
+            if ok(k):
+                st_qk(k, 1, 1)
+            if ok(k - 1):
+                st_et(k - 1, 0)
+            if ok(k):
+                st_w1(k, 0, 1)
+            if ok(k + 1):
+                st_qk(k + 1, 0, 0)
+            if ok(k - 1):
+                st_et(k - 1, 1)
+            if ok(k):
+                st_w2(k, 0, 0)
+                st_w2(k, 0, 1)
+                st_w1(k, 1, 0)
+            if ok(k + 1):
+                st_qk(k + 1, 0, 1)
+            if ok(k + 2):
+                st_qt(k + 2)
+            if ok(k - 3):
+                st_pv(k - 3, 0)
+                st_pv(k - 3, 1)
+            elif k == 0:
+                kt0 = prepare_keys(1, 0, "pv", 2)
+                kt1 = prepare_keys(1, 1, "pv", 2)
+            if ok(k):
+                st_w1(k, 1, 1)
+            if ok(k + 1):
+                st_qk(k + 1, 1, 0)
+            if ok(k):
+                st_w2(k, 1, 0)
+            if ok(k + 1):
+                st_w1(k + 1, 0, 0)
+            if ok(k):
+                st_w2(k, 1, 1)
+                st_w3(k, 0, 0)
+            if ok(k - 1):
+                st_w4(k - 1, 0)
+                st_w4(k - 1, 1)
+            elif k == 0:
+                nc.scalar.copy(out=k_t[1][0][:], in_=kt0[:])
+                nc.scalar.copy(out=k_t[1][1][:], in_=kt1[:])
+            if ok(k):
+                st_w3(k, 0, 1)

@@ -96,11 +96,48 @@ def tile_dsattention_t_kernel(tc, queries, keys, values, tau, delta, out):
         def quantise_values(b):
             nc.vector.quantize_mx(out=v_codes[b][:].bitcast(FP8X4), scales=v_scales[b][:], in_=grp[b][:])
 
-        kt0 = prepare_keys(0, 0, "sc", 3)
-        nc.scalar.copy(out=k_t[0][0][:], in_=kt0[:])
-        kt1 = prepare_keys(0, 1, "sc", 3)
-        nc.vector.tensor_copy(out=k_t[0][1][:], in_=kt1[:])
         grp = [regroup_values(b) for b in range(B)]
+
+        ones_bf = const.tile([P, P], BF16, name="ones_bf")
+        nc.gpsimd.memset(ones_bf[:], 1.0)
+        itau = const.tile([P, B], F32, name="itau")
+        hi_b = const.tile([P, B], BF16, name="hi_b")
+        mid_b = const.tile([P, B], BF16, name="mid_b")
+        lo_b = const.tile([P, B], BF16, name="lo_b")
+        r_1 = const.tile([P, B], F32, name="r_1")
+        r_2 = const.tile([P, B], F32, name="r_2")
+        c_0 = const.tile([P, B], F32, name="c_0")
+        c_1 = const.tile([P, B], F32, name="c_1")
+        c_2 = const.tile([P, B], F32, name="c_2")
+        w_d = [const.tile([P, P], BF16, name="w_d%d" % b) for b in range(B)]
+        small = [
+            lambda: nc.vector.reciprocal(out=itau[:], in_=tau_bf[:]),
+            lambda: nc.vector.tensor_copy(out=hi_b[:], in_=itau[:]),
+            lambda: nc.vector.tensor_tensor(out=r_1[:], in0=itau[:], in1=hi_b[:], op=ALU.subtract),
+            lambda: nc.vector.tensor_copy(out=mid_b[:], in_=r_1[:]),
+            lambda: nc.vector.tensor_tensor(out=r_2[:], in0=r_1[:], in1=mid_b[:], op=ALU.subtract),
+            lambda: nc.vector.tensor_copy(out=lo_b[:], in_=r_2[:]),
+            lambda: nc.vector.tensor_scalar_mul(out=c_0[:], in0=hi_b[:], scalar1=ident_f[:, 0:1]),
+            lambda: nc.vector.scalar_tensor_tensor(
+                out=c_1[:], in0=mid_b[:], scalar=ident_f[:, 1:2], in1=c_0[:], op0=ALU.mult, op1=ALU.add),
+            lambda: nc.vector.scalar_tensor_tensor(
+                out=c_2[:], in0=lo_b[:], scalar=ident_f[:, 2:3], in1=c_1[:], op0=ALU.mult, op1=ALU.add),
+            lambda: nc.vector.tensor_scalar_mul(out=w_d[0][:], in0=ones_bf[:], scalar1=c_2[:, 0:1]),
+            lambda: nc.vector.tensor_scalar_mul(out=w_d[1][:], in0=ones_bf[:], scalar1=c_2[:, 1:2]),
+        ]
+
+        done_small = [0]
+
+        def one_small():
+            if done_small[0] < len(small):
+                small[done_small[0]]()
+                done_small[0] += 1
+
+        def on_pe(k, u, h):
+            return u == 1 and h == 1 and 3 <= k < 28
+
+        def w6_on_vector(k, u):
+            return u == 1 and k % 2 == 0
 
         qt_ps, q_t, sc, nz, mn, rs, e_sb, et, et_sb, g, codes, scl, rinv, pv, o_sb = (
             {}, {}, {}, {}, {}, {}, {}, {}, {}, {}, {}, {}, {}, {}, {})
@@ -120,7 +157,10 @@ def tile_dsattention_t_kernel(tc, queries, keys, values, tau, delta, out):
 
         def st_w7(k):
             q_t[k] = work.tile([P, 4 * P], F32, name="q_t", tag="q_t", bufs=3)
-            nc.scalar.copy(out=q_t[k][:], in_=qt_ps[k][:])
+            if k == 0:
+                nc.vector.tensor_copy(out=q_t[k][:], in_=qt_ps[k][:])
+            else:
+                nc.scalar.copy(out=q_t[k][:], in_=qt_ps[k][:])
 
         def st_qk(k, u, h):
             m = 2 * k + u
@@ -129,26 +169,39 @@ def tile_dsattention_t_kernel(tc, queries, keys, values, tau, delta, out):
             qv = q_t[k][:].bitcast(BF16).rearrange("p (i l e) -> p i l e", i=4, e=2)
             kv = k_t[b][h][:].bitcast(BF16).rearrange("p (s e) -> p s e", e=2)
             for e in range(2):
-                nc.tensor.matmul(sc[m, h][:], lhsT=qv[:, u * H + h, :, e], rhs=kv[:, :, e], start=(e == 0), stop=(e == 1))
+                nc.tensor.matmul(
+                    sc[m, h][:], lhsT=qv[:, u * H + h, :, e], rhs=kv[:, :, e], start=(e == 0),
+                    stop=(e == 1 and not on_pe(k, u, h)))
+            if on_pe(k, u, h):
+                nc.tensor.matmul(sc[m, h][:], lhsT=w_d[b][:], rhs=delta_bf[:, b * S:(b + 1) * S], start=False, stop=True)
 
         def st_w1(k, u, h):
             m = 2 * k + u
             b = m // J
-            nz[m, h] = work.tile([P, S], F32, name="nz", tag="nz", bufs=6)
-            nc.vector.scalar_tensor_tensor(
-                out=nz[m, h][:], in0=sc[m, h][:], scalar=ntau[:, b:b + 1],
-                in1=ndelta[:, b * S:(b + 1) * S], op0=ALU.mult, op1=ALU.add)
+            nz[m, h] = work.tile([P, S], F32, name="nz", tag="nz", bufs=10)
+            if on_pe(k, u, h):
+                mn[m, h] = work.tile([P, 1], F32, name="mn", tag="mn", bufs=12)
+                nc.vector.tensor_scalar(
+                    out=nz[m, h][:], in0=sc[m, h][:], scalar1=ntau[:, b:b + 1], scalar2=None,
+                    op0=ALU.mult, op1=ALU.min, accum_out=mn[m, h][:])
+            else:
+                nc.vector.scalar_tensor_tensor(
+                    out=nz[m, h][:], in0=sc[m, h][:], scalar=ntau[:, b:b + 1],
+                    in1=ndelta[:, b * S:(b + 1) * S], op0=ALU.mult, op1=ALU.add)
+            one_small()
 
         def st_w2(k, u, h):
             m = 2 * k + u
-            mn[m, h] = work.tile([P, 1], F32, name="mn", tag="mn", bufs=8)
+            if on_pe(k, u, h):
+                return
+            mn[m, h] = work.tile([P, 1], F32, name="mn", tag="mn", bufs=12)
             nc.vector.tensor_reduce(out=mn[m, h][:], in_=nz[m, h][:], axis=AX.X, op=ALU.min)
 
         def st_w3(k, u, h):
             m = 2 * k + u
             if u == 0 and h == 0:
                 rs[k] = work.tile([P, 4], F32, name="rs", tag="rs", bufs=5)
-            if h == 0:
+            if m not in e_sb:
                 e_sb[m] = work.tile([P, H * S], BF16, name="e_sb", tag="e_sb", bufs=4)
             i = u * H + h
             nc.scalar.activation(
@@ -202,24 +255,36 @@ def tile_dsattention_t_kernel(tc, queries, keys, values, tau, delta, out):
                 o_sb[k] = work.tile([P, 4 * D], F32, name="o_sb", tag="o_sb", bufs=3)
             for h in (1, 0):
                 i = u * H + h
-                nc.scalar.activation(
-                    out=o_sb[k][:, i * D:(i + 1) * D], in_=pv[m][:, h * D:(h + 1) * D], func=ACT.Copy,
-                    scale=rinv[k][:, i:i + 1])
+                if w6_on_vector(k, u):
+                    nc.vector.tensor_scalar_mul(
+                        out=o_sb[k][:, i * D:(i + 1) * D], in0=pv[m][:, h * D:(h + 1) * D], scalar1=rinv[k][:, i:i + 1])
+                else:
+                    nc.scalar.activation(
+                        out=o_sb[k][:, i * D:(i + 1) * D], in_=pv[m][:, h * D:(h + 1) * D], func=ACT.Copy,
+                        scale=rinv[k][:, i:i + 1])
             if u == 1:
                 b, j = m // J, m % J
                 nc.sync.dma_start(
                     out=out[b].rearrange("(p j) h d -> p j (h d)", j=J)[:, j - 1:j + 1, :],
                     in_=o_sb[k][:].rearrange("p (j c) -> p j c", j=2))
 
-        for k in range(-2, QUADS + 4):
-            if ok(k + 1):
+        kt0 = prepare_keys(0, 0, "sc", 3)
+        st_qt(0)
+        nc.scalar.copy(out=k_t[0][0][:], in_=kt0[:])
+        kt1 = prepare_keys(0, 1, "sc", 3)
+        st_w7(0)
+        nc.scalar.copy(out=k_t[0][1][:], in_=kt1[:])
+
+        for k in range(-1, QUADS + 4):
+            if ok(k + 1) and k + 1 > 0:
                 st_w7(k + 1)
             if ok(k - 1):
-                st_w3(k - 1, 1, 0)
                 st_w3(k - 1, 1, 1)
+                st_w3(k - 1, 1, 0)
             if ok(k - 4):
                 st_w6(k - 4, 0)
-                st_w6(k - 4, 1)
+                if not w6_on_vector(k - 4, 1):
+                    st_w6(k - 4, 1)
             if ok(k - 3):
                 st_w5(k - 3)
             elif k in (0, 1):
@@ -233,6 +298,8 @@ def tile_dsattention_t_kernel(tc, queries, keys, values, tau, delta, out):
                 st_et(k - 1, 0)
             if ok(k):
                 st_w1(k, 0, 1)
+            if ok(k - 4) and w6_on_vector(k - 4, 1):
+                st_w6(k - 4, 1)
             if ok(k + 1):
                 st_qk(k + 1, 0, 0)
             if ok(k - 1):
@@ -255,18 +322,18 @@ def tile_dsattention_t_kernel(tc, queries, keys, values, tau, delta, out):
                 st_w1(k, 1, 1)
             if ok(k + 1):
                 st_qk(k + 1, 1, 0)
-            if ok(k):
-                st_w2(k, 1, 0)
-            if ok(k + 1):
                 st_w1(k + 1, 0, 0)
             if ok(k):
+                st_w2(k, 1, 0)
                 st_w2(k, 1, 1)
                 st_w3(k, 0, 0)
             if ok(k - 1):
                 st_w4(k - 1, 0)
-                st_w4(k - 1, 1)
             elif k == 0:
                 nc.scalar.copy(out=k_t[1][0][:], in_=kt0[:])
-                nc.scalar.copy(out=k_t[1][1][:], in_=kt1[:])
             if ok(k):
                 st_w3(k, 0, 1)
+            if ok(k - 1):
+                st_w4(k - 1, 1)
+            elif k == 0:
+                nc.scalar.copy(out=k_t[1][1][:], in_=kt1[:])

@@ -110,8 +110,12 @@ def tile_dsattention_t_kernel(tc, queries, keys, values, tau, delta, out):
         c_1 = const.tile([P, B], F32, name="c_1")
         c_2 = const.tile([P, B], F32, name="c_2")
         w_d = [const.tile([P, P], BF16, name="w_d%d" % b) for b in range(B)]
+        dtau = const.tile([P, B * S], F32, name="dtau")
+        d_t = const.tile([P, B * S], F32, name="d_t")
         small = [
             lambda: nc.vector.reciprocal(out=itau[:], in_=tau_bf[:]),
+            lambda: nc.vector.tensor_scalar_mul(out=dtau[:, 0:S], in0=delta_bf[:, 0:S], scalar1=itau[:, 0:1]),
+            lambda: nc.vector.tensor_scalar_mul(out=dtau[:, S:2 * S], in0=delta_bf[:, S:2 * S], scalar1=itau[:, 1:2]),
             lambda: nc.vector.tensor_copy(out=hi_b[:], in_=itau[:]),
             lambda: nc.vector.tensor_tensor(out=r_1[:], in0=itau[:], in1=hi_b[:], op=ALU.subtract),
             lambda: nc.vector.tensor_copy(out=mid_b[:], in_=r_1[:]),
@@ -133,11 +137,24 @@ def tile_dsattention_t_kernel(tc, queries, keys, values, tau, delta, out):
                 small[done_small[0]]()
                 done_small[0] += 1
 
-        def on_pe(k, u, h):
+        def by_matmul(k, u, h):
             return u == 1 and h == 1 and 3 <= k < 28
 
+        def by_transpose(k, u, h):
+            return h == 1 and k >= 3 and ((u == 1 and k >= 28) or (u == 0 and k % 2 == 1))
+
+        def on_pe(k, u, h):
+            return by_matmul(k, u, h) or by_transpose(k, u, h)
+
         def w6_on_vector(k, u):
-            return u == 1 and k % 2 == 0
+            return u == 1 and k % 3 != 2
+
+        def spread_delta(b):
+            dt_ps = psum.tile([P, S], F32, name="dt_ps", tag="pv", bufs=2)
+            for t in range(4):
+                c0 = b * S + t * P
+                nc.tensor.transpose(dt_ps[:, t * P:(t + 1) * P], dtau[:, c0:c0 + P], ident_f[:])
+            return dt_ps
 
         qt_ps, q_t, sc, nz, mn, rs, e_sb, et, et_sb, g, codes, scl, rinv, pv, o_sb = (
             {}, {}, {}, {}, {}, {}, {}, {}, {}, {}, {}, {}, {}, {}, {})
@@ -172,8 +189,14 @@ def tile_dsattention_t_kernel(tc, queries, keys, values, tau, delta, out):
                 nc.tensor.matmul(
                     sc[m, h][:], lhsT=qv[:, u * H + h, :, e], rhs=kv[:, :, e], start=(e == 0),
                     stop=(e == 1 and not on_pe(k, u, h)))
-            if on_pe(k, u, h):
+            if by_matmul(k, u, h):
                 nc.tensor.matmul(sc[m, h][:], lhsT=w_d[b][:], rhs=delta_bf[:, b * S:(b + 1) * S], start=False, stop=True)
+            if by_transpose(k, u, h):
+                for t in range(4):
+                    c0 = b * S + t * P
+                    nc.tensor.matmul(
+                        sc[m, h][:, t * P:(t + 1) * P], lhsT=d_t[:, c0:c0 + P], rhs=ident_f[:], is_transpose=True,
+                        start=False, stop=(t == 3))
 
         def st_w1(k, u, h):
             m = 2 * k + u
@@ -199,14 +222,15 @@ def tile_dsattention_t_kernel(tc, queries, keys, values, tau, delta, out):
 
         def st_w3(k, u, h):
             m = 2 * k + u
-            if u == 0 and h == 0:
-                rs[k] = work.tile([P, 4], F32, name="rs", tag="rs", bufs=5)
+            o = k // 2
+            if k % 2 == 0 and u == 0 and h == 0:
+                rs[o] = work.tile([P, 8], F32, name="rs", tag="rs", bufs=4)
             if m not in e_sb:
                 e_sb[m] = work.tile([P, H * S], BF16, name="e_sb", tag="e_sb", bufs=4)
-            i = u * H + h
+            i = (k % 2) * 4 + u * H + h
             nc.scalar.activation(
                 out=e_sb[m][:, h * S:(h + 1) * S], in_=nz[m, h][:], func=ACT.Exp, bias=mn[m, h][:], scale=-1.0,
-                accum_out=rs[k][:, i:i + 1])
+                accum_out=rs[o][:, i:i + 1])
 
         def st_et(k, u):
             m = 2 * k + u
@@ -216,35 +240,38 @@ def tile_dsattention_t_kernel(tc, queries, keys, values, tau, delta, out):
 
         def st_w4(k, u):
             m = 2 * k + u
-            et_sb[m] = work.tile([P, H * S], BF16, name="et_sb", tag="et_sb", bufs=3)
+            et_sb[m] = work.tile([P, H * S], BF16, name="et_sb", tag="et_sb", bufs=8)
             nc.scalar.copy(out=et_sb[m][:], in_=et[m][:])
 
         def st_rg(k, u):
             m = 2 * k + u
-            if u == 0:
-                g[k] = work.tile([P, 2 * H * S], BF16, name="g", tag="g", bufs=1, align_bytes=64)
+            o = k // 2
+            if k % 2 == 0 and u == 0:
+                g[o] = work.tile([P, 4 * H * S], BF16, name="g", tag="g", bufs=1, align_bytes=64)
+            c0 = ((k % 2) * 2 + u) * H * S
             nc.gpsimd.tensor_scalar(
-                out=g[k][:, u * H * S:(u + 1) * H * S].rearrange("p (h l t) -> p h l t", h=H, t=4),
+                out=g[o][:, c0:c0 + H * S].rearrange("p (h l t) -> p h l t", h=H, t=4),
                 in0=et_sb[m][:].rearrange("p (h t l) -> p h l t", h=H, t=4),
                 scalar1=1.0, scalar2=0.0, op0=ALU.mult, op1=ALU.add)
 
-        def st_w5(k):
-            codes[k] = work.tile([P, 4 * P], U32, name="codes", tag="codes", bufs=2, align_bytes=64)
-            scl[k] = work.tile([P, 4 * P], U8, name="scl", tag="scl", bufs=2, align_bytes=64)
-            nc.vector.quantize_mx(out=codes[k][:].bitcast(FP8X4), scales=scl[k][:], in_=g[k][:])
-            rinv[k] = work.tile([P, 4], F32, name="rinv", tag="rinv", bufs=3)
-            nc.vector.reciprocal(out=rinv[k][:], in_=rs[k][:])
+        def st_w5(o):
+            codes[o] = work.tile([P, 8 * P], U32, name="codes", tag="codes", bufs=2, align_bytes=64)
+            scl[o] = work.tile([P, 8 * P], U8, name="scl", tag="scl", bufs=2, align_bytes=64)
+            nc.vector.quantize_mx(out=codes[o][:].bitcast(FP8X4), scales=scl[o][:], in_=g[o][:])
+            rinv[o] = work.tile([P, 8], F32, name="rinv", tag="rinv", bufs=3)
+            nc.vector.reciprocal(out=rinv[o][:], in_=rs[o][:])
 
         def st_pv(k, u):
             m = 2 * k + u
             b = m // J
             pv[m] = psum.tile([P, H * D], F32, name="pv", tag="pv", bufs=2)
+            o = k // 2
             for h in range(H):
-                i = u * H + h
+                i = (k % 2) * 4 + u * H + h
                 nc.tensor.matmul_mx(
                     out=pv[m][:, h * D:(h + 1) * D],
-                    lhsT=codes[k][:, i * P:(i + 1) * P].bitcast(FP8X4),
-                    lhsT_scale=scl[k][:, i * P:(i + 1) * P],
+                    lhsT=codes[o][:, i * P:(i + 1) * P].bitcast(FP8X4),
+                    lhsT_scale=scl[o][:, i * P:(i + 1) * P],
                     rhs=v_codes[b][:, h * D:(h + 1) * D].bitcast(FP8X4),
                     rhs_scale=v_scales[b][:, h * D:(h + 1) * D],
                     start=True, stop=True)
@@ -255,13 +282,13 @@ def tile_dsattention_t_kernel(tc, queries, keys, values, tau, delta, out):
                 o_sb[k] = work.tile([P, 4 * D], F32, name="o_sb", tag="o_sb", bufs=3)
             for h in (1, 0):
                 i = u * H + h
+                r = rinv[k // 2][:, (k % 2) * 4 + i:(k % 2) * 4 + i + 1]
                 if w6_on_vector(k, u):
                     nc.vector.tensor_scalar_mul(
-                        out=o_sb[k][:, i * D:(i + 1) * D], in0=pv[m][:, h * D:(h + 1) * D], scalar1=rinv[k][:, i:i + 1])
+                        out=o_sb[k][:, i * D:(i + 1) * D], in0=pv[m][:, h * D:(h + 1) * D], scalar1=r)
                 else:
                     nc.scalar.activation(
-                        out=o_sb[k][:, i * D:(i + 1) * D], in_=pv[m][:, h * D:(h + 1) * D], func=ACT.Copy,
-                        scale=rinv[k][:, i:i + 1])
+                        out=o_sb[k][:, i * D:(i + 1) * D], in_=pv[m][:, h * D:(h + 1) * D], func=ACT.Copy, scale=r)
             if u == 1:
                 b, j = m // J, m % J
                 nc.sync.dma_start(
@@ -276,64 +303,73 @@ def tile_dsattention_t_kernel(tc, queries, keys, values, tau, delta, out):
         nc.scalar.copy(out=k_t[0][1][:], in_=kt1[:])
 
         for k in range(-1, QUADS + 4):
+            closes = ok(k - 3) and (k - 3) % 2 == 1
             if ok(k + 1) and k + 1 > 0:
                 st_w7(k + 1)
             if ok(k - 1):
-                st_w3(k - 1, 1, 1)
                 st_w3(k - 1, 1, 0)
-            if ok(k - 4):
-                st_w6(k - 4, 0)
-                if not w6_on_vector(k - 4, 1):
-                    st_w6(k - 4, 1)
-            if ok(k - 3):
-                st_w5(k - 3)
+                st_w3(k - 1, 1, 1)
+            if closes:
+                st_w5((k - 3) // 2)
+                st_pv(k - 4, 0)
+                st_pv(k - 4, 1)
             elif k in (0, 1):
                 quantise_values(k)
             if ok(k - 2):
                 st_rg(k - 2, 0)
                 st_rg(k - 2, 1)
+            if ok(k - 4):
+                st_w6(k - 4, 0)
             if ok(k):
                 st_qk(k, 1, 1)
-            if ok(k - 1):
-                st_et(k - 1, 0)
-            if ok(k):
                 st_w1(k, 0, 1)
-            if ok(k - 4) and w6_on_vector(k - 4, 1):
-                st_w6(k - 4, 1)
             if ok(k + 1):
                 st_qk(k + 1, 0, 0)
             if ok(k - 1):
-                st_et(k - 1, 1)
+                st_et(k - 1, 0)
             if ok(k):
                 st_w2(k, 0, 0)
-                st_w2(k, 0, 1)
                 st_w1(k, 1, 0)
             if ok(k + 1):
                 st_qk(k + 1, 0, 1)
+            if ok(k - 1):
+                st_et(k - 1, 1)
             if ok(k + 2):
                 st_qt(k + 2)
-            if ok(k - 3):
-                st_pv(k - 3, 0)
-                st_pv(k - 3, 1)
-            elif k == 0:
-                kt0 = prepare_keys(1, 0, "pv", 2)
-                kt1 = prepare_keys(1, 1, "pv", 2)
+            if ok(k):
+                st_w2(k, 0, 1)
+            if ok(k - 4) and w6_on_vector(k - 4, 1):
+                st_w6(k - 4, 1)
             if ok(k):
                 st_w1(k, 1, 1)
             if ok(k + 1):
                 st_qk(k + 1, 1, 0)
-                st_w1(k + 1, 0, 0)
             if ok(k):
-                st_w2(k, 1, 0)
-                st_w2(k, 1, 1)
                 st_w3(k, 0, 0)
             if ok(k - 1):
                 st_w4(k - 1, 0)
             elif k == 0:
+                kt0 = prepare_keys(1, 0, "pv", 2)
                 nc.scalar.copy(out=k_t[1][0][:], in_=kt0[:])
+            if k == 1:
+                kt0 = spread_delta(0)
+                nc.scalar.copy(out=d_t[:, 0:S], in_=kt0[:])
+            if ok(k - 4) and not w6_on_vector(k - 4, 1):
+                st_w6(k - 4, 1)
+            if closes:
+                st_pv(k - 3, 0)
+                st_pv(k - 3, 1)
+            if ok(k + 1):
+                st_w1(k + 1, 0, 0)
             if ok(k):
+                st_w2(k, 1, 0)
+                st_w2(k, 1, 1)
                 st_w3(k, 0, 1)
             if ok(k - 1):
                 st_w4(k - 1, 1)
             elif k == 0:
+                kt1 = prepare_keys(1, 1, "pv", 2)
                 nc.scalar.copy(out=k_t[1][1][:], in_=kt1[:])
+            if k == 1:
+                kt1 = spread_delta(1)
+                nc.scalar.copy(out=d_t[:, S:2 * S], in_=kt1[:])

@@ -162,15 +162,44 @@ def tile_dsattention_t_kernel(tc, queries, keys, values, tau, delta, out):
         def ok(k):
             return 0 <= k < QUADS
 
+        pending = []
+        emitted = [0]
+
+        def weave(count):
+            for i in range(count):
+                if emitted[0] < len(pending):
+                    pending[emitted[0]]()
+                    emitted[0] += 1
+
+        def flush():
+            weave(len(pending) - emitted[0])
+
+        def qt_one(k, i):
+            if i == 0:
+                qt_ps[k] = psum.tile([P, 4 * P], F32, name="qt_ps", tag="qt", bufs=1)
+            m = 2 * k + i // H
+            words = q_sb[m // J][:].bitcast(F32)
+            c0 = (m % J) * (H * D // 2) + (i % H) * (D // 2)
+            nc.tensor.transpose(qt_ps[k][:, i * P:(i + 1) * P], words[:, c0:c0 + P], ident_f[:])
+
         def st_qt(k):
-            qt_ps[k] = psum.tile([P, 4 * P], F32, name="qt_ps", tag="qt", bufs=1)
-            for u in range(2):
-                m = 2 * k + u
-                words = q_sb[m // J][:].bitcast(F32)
-                for h in range(H):
-                    c0 = (m % J) * (H * D // 2) + h * (D // 2)
-                    i = u * H + h
-                    nc.tensor.transpose(qt_ps[k][:, i * P:(i + 1) * P], words[:, c0:c0 + P], ident_f[:])
+            for i in range(4):
+                qt_one(k, i)
+
+        def et_one(m, i):
+            if i == 0:
+                et[m] = psum.tile([P, H * S], BF16, name="et", tag="et", bufs=2)
+            nc.tensor.transpose(et[m][:, i * P:(i + 1) * P], e_sb[m][:, i * P:(i + 1) * P], ident_b[:])
+
+        def plan_et(k, u):
+            for i in range(8):
+                pending.append(lambda m=2 * k + u, i=i: et_one(m, i))
+
+        def plan_et_qt(k, u, kq):
+            for i in range(8):
+                pending.append(lambda m=2 * k + u, i=i: et_one(m, i))
+                if i % 2 == 1 and ok(kq):
+                    pending.append(lambda i=i: qt_one(kq, i // 2))
 
         def st_w7(k):
             q_t[k] = work.tile([P, 4 * P], F32, name="q_t", tag="q_t", bufs=3)
@@ -179,16 +208,20 @@ def tile_dsattention_t_kernel(tc, queries, keys, values, tau, delta, out):
             else:
                 nc.scalar.copy(out=q_t[k][:], in_=qt_ps[k][:])
 
-        def st_qk(k, u, h):
+        def st_qk(k, u, h, lead, count):
             m = 2 * k + u
             b = m // J
             sc[m, h] = psum.tile([P, S], F32, name="sc", tag="sc", bufs=3)
             qv = q_t[k][:].bitcast(BF16).rearrange("p (i l e) -> p i l e", i=4, e=2)
             kv = k_t[b][h][:].bitcast(BF16).rearrange("p (s e) -> p s e", e=2)
             for e in range(2):
+                if lead:
+                    weave(count)
                 nc.tensor.matmul(
                     sc[m, h][:], lhsT=qv[:, u * H + h, :, e], rhs=kv[:, :, e], start=(e == 0),
                     stop=(e == 1 and not on_pe(k, u, h)))
+                if e == 0 and not lead:
+                    weave(count)
             if by_matmul(k, u, h):
                 nc.tensor.matmul(sc[m, h][:], lhsT=w_d[b][:], rhs=delta_bf[:, b * S:(b + 1) * S], start=False, stop=True)
             if by_transpose(k, u, h):
@@ -197,6 +230,8 @@ def tile_dsattention_t_kernel(tc, queries, keys, values, tau, delta, out):
                     nc.tensor.matmul(
                         sc[m, h][:, t * P:(t + 1) * P], lhsT=d_t[:, c0:c0 + P], rhs=ident_f[:], is_transpose=True,
                         start=False, stop=(t == 3))
+            if not lead:
+                weave(count)
 
         def st_w1(k, u, h):
             m = 2 * k + u
@@ -231,12 +266,6 @@ def tile_dsattention_t_kernel(tc, queries, keys, values, tau, delta, out):
             nc.scalar.activation(
                 out=e_sb[m][:, h * S:(h + 1) * S], in_=nz[m, h][:], func=ACT.Exp, bias=mn[m, h][:], scale=-1.0,
                 accum_out=rs[o][:, i:i + 1])
-
-        def st_et(k, u):
-            m = 2 * k + u
-            et[m] = psum.tile([P, H * S], BF16, name="et", tag="et", bufs=2)
-            for i in range(8):
-                nc.tensor.transpose(et[m][:, i * P:(i + 1) * P], e_sb[m][:, i * P:(i + 1) * P], ident_b[:])
 
         def st_w4(k, u):
             m = 2 * k + u
@@ -320,22 +349,23 @@ def tile_dsattention_t_kernel(tc, queries, keys, values, tau, delta, out):
                 st_rg(k - 2, 1)
             if ok(k - 4):
                 st_w6(k - 4, 0)
+            if ok(k - 1):
+                plan_et(k - 1, 0)
             if ok(k):
-                st_qk(k, 1, 1)
+                st_qk(k, 1, 1, False, 2)
                 st_w1(k, 0, 1)
             if ok(k + 1):
-                st_qk(k + 1, 0, 0)
-            if ok(k - 1):
-                st_et(k - 1, 0)
+                st_qk(k + 1, 0, 0, False, 2)
+            flush()
             if ok(k):
                 st_w2(k, 0, 0)
                 st_w1(k, 1, 0)
-            if ok(k + 1):
-                st_qk(k + 1, 0, 1)
             if ok(k - 1):
-                st_et(k - 1, 1)
-            if ok(k + 2):
+                plan_et_qt(k - 1, 1, k + 2)
+            elif ok(k + 2):
                 st_qt(k + 2)
+            if ok(k + 1):
+                st_qk(k + 1, 0, 1, False, 3)
             if ok(k):
                 st_w2(k, 0, 1)
             if ok(k - 4) and w6_on_vector(k - 4, 1):
@@ -343,7 +373,8 @@ def tile_dsattention_t_kernel(tc, queries, keys, values, tau, delta, out):
             if ok(k):
                 st_w1(k, 1, 1)
             if ok(k + 1):
-                st_qk(k + 1, 1, 0)
+                st_qk(k + 1, 1, 0, True, 3)
+            flush()
             if ok(k):
                 st_w3(k, 0, 0)
             if ok(k - 1):

@@ -147,7 +147,10 @@ def tile_dsattention_t_kernel(tc, queries, keys, values, tau, delta, out):
             return by_matmul(k, u, h) or by_transpose(k, u, h)
 
         def w6_on_vector(k, u):
-            return u == 1 and k % 3 != 2
+            return u == 1 and (k % 3 != 2 or k >= QUADS - 4)
+
+        def direct(k):
+            return k >= QUADS - 2
 
         def spread_delta(b):
             dt_ps = psum.tile([P, S], F32, name="dt_ps", tag="pv", bufs=2)
@@ -156,50 +159,21 @@ def tile_dsattention_t_kernel(tc, queries, keys, values, tau, delta, out):
                 nc.tensor.transpose(dt_ps[:, t * P:(t + 1) * P], dtau[:, c0:c0 + P], ident_f[:])
             return dt_ps
 
-        qt_ps, q_t, sc, nz, mn, rs, e_sb, et, et_sb, g, codes, scl, rinv, pv, o_sb = (
-            {}, {}, {}, {}, {}, {}, {}, {}, {}, {}, {}, {}, {}, {}, {})
+        qt_ps, q_t, sc, nz, mn, rs, e_sb, et, et_sb, g, codes, scl, rinv, pv, o_sb, g_2 = (
+            {}, {}, {}, {}, {}, {}, {}, {}, {}, {}, {}, {}, {}, {}, {}, {})
 
         def ok(k):
             return 0 <= k < QUADS
 
-        pending = []
-        emitted = [0]
-
-        def weave(count):
-            for i in range(count):
-                if emitted[0] < len(pending):
-                    pending[emitted[0]]()
-                    emitted[0] += 1
-
-        def flush():
-            weave(len(pending) - emitted[0])
-
-        def qt_one(k, i):
-            if i == 0:
-                qt_ps[k] = psum.tile([P, 4 * P], F32, name="qt_ps", tag="qt", bufs=1)
-            m = 2 * k + i // H
-            words = q_sb[m // J][:].bitcast(F32)
-            c0 = (m % J) * (H * D // 2) + (i % H) * (D // 2)
-            nc.tensor.transpose(qt_ps[k][:, i * P:(i + 1) * P], words[:, c0:c0 + P], ident_f[:])
-
         def st_qt(k):
-            for i in range(4):
-                qt_one(k, i)
-
-        def et_one(m, i):
-            if i == 0:
-                et[m] = psum.tile([P, H * S], BF16, name="et", tag="et", bufs=2)
-            nc.tensor.transpose(et[m][:, i * P:(i + 1) * P], e_sb[m][:, i * P:(i + 1) * P], ident_b[:])
-
-        def plan_et(k, u):
-            for i in range(8):
-                pending.append(lambda m=2 * k + u, i=i: et_one(m, i))
-
-        def plan_et_qt(k, u, kq):
-            for i in range(8):
-                pending.append(lambda m=2 * k + u, i=i: et_one(m, i))
-                if i % 2 == 1 and ok(kq):
-                    pending.append(lambda i=i: qt_one(kq, i // 2))
+            qt_ps[k] = psum.tile([P, 4 * P], F32, name="qt_ps", tag="qt", bufs=1)
+            for u in range(2):
+                m = 2 * k + u
+                words = q_sb[m // J][:].bitcast(F32)
+                for h in range(H):
+                    c0 = (m % J) * (H * D // 2) + h * (D // 2)
+                    i = u * H + h
+                    nc.tensor.transpose(qt_ps[k][:, i * P:(i + 1) * P], words[:, c0:c0 + P], ident_f[:])
 
         def st_w7(k):
             q_t[k] = work.tile([P, 4 * P], F32, name="q_t", tag="q_t", bufs=3)
@@ -208,20 +182,16 @@ def tile_dsattention_t_kernel(tc, queries, keys, values, tau, delta, out):
             else:
                 nc.scalar.copy(out=q_t[k][:], in_=qt_ps[k][:])
 
-        def st_qk(k, u, h, lead, count):
+        def st_qk(k, u, h):
             m = 2 * k + u
             b = m // J
             sc[m, h] = psum.tile([P, S], F32, name="sc", tag="sc", bufs=3)
             qv = q_t[k][:].bitcast(BF16).rearrange("p (i l e) -> p i l e", i=4, e=2)
             kv = k_t[b][h][:].bitcast(BF16).rearrange("p (s e) -> p s e", e=2)
             for e in range(2):
-                if lead:
-                    weave(count)
                 nc.tensor.matmul(
                     sc[m, h][:], lhsT=qv[:, u * H + h, :, e], rhs=kv[:, :, e], start=(e == 0),
                     stop=(e == 1 and not on_pe(k, u, h)))
-                if e == 0 and not lead:
-                    weave(count)
             if by_matmul(k, u, h):
                 nc.tensor.matmul(sc[m, h][:], lhsT=w_d[b][:], rhs=delta_bf[:, b * S:(b + 1) * S], start=False, stop=True)
             if by_transpose(k, u, h):
@@ -230,8 +200,6 @@ def tile_dsattention_t_kernel(tc, queries, keys, values, tau, delta, out):
                     nc.tensor.matmul(
                         sc[m, h][:, t * P:(t + 1) * P], lhsT=d_t[:, c0:c0 + P], rhs=ident_f[:], is_transpose=True,
                         start=False, stop=(t == 3))
-            if not lead:
-                weave(count)
 
         def st_w1(k, u, h):
             m = 2 * k + u
@@ -257,50 +225,79 @@ def tile_dsattention_t_kernel(tc, queries, keys, values, tau, delta, out):
 
         def st_w3(k, u, h):
             m = 2 * k + u
-            o = k // 2
-            if k % 2 == 0 and u == 0 and h == 0:
-                rs[o] = work.tile([P, 8], F32, name="rs", tag="rs", bufs=4)
+            if u == 0 and h == 0:
+                rs[k] = work.tile([P, 4], F32, name="rs", tag="rs", bufs=5)
             if m not in e_sb:
                 e_sb[m] = work.tile([P, H * S], BF16, name="e_sb", tag="e_sb", bufs=4)
-            i = (k % 2) * 4 + u * H + h
+            i = u * H + h
             nc.scalar.activation(
                 out=e_sb[m][:, h * S:(h + 1) * S], in_=nz[m, h][:], func=ACT.Exp, bias=mn[m, h][:], scale=-1.0,
-                accum_out=rs[o][:, i:i + 1])
+                accum_out=rs[k][:, i:i + 1])
+
+        def st_et(k, u):
+            m = 2 * k + u
+            et[m] = psum.tile([P, H * S], BF16, name="et", tag="et", bufs=2)
+            for i in range(8):
+                nc.tensor.transpose(et[m][:, i * P:(i + 1) * P], e_sb[m][:, i * P:(i + 1) * P], ident_b[:])
 
         def st_w4(k, u):
             m = 2 * k + u
-            et_sb[m] = work.tile([P, H * S], BF16, name="et_sb", tag="et_sb", bufs=8)
+            et_sb[m] = work.tile([P, H * S], BF16, name="et_sb", tag="et_sb", bufs=3)
             nc.scalar.copy(out=et_sb[m][:], in_=et[m][:])
 
         def st_rg(k, u):
             m = 2 * k + u
-            o = k // 2
-            if k % 2 == 0 and u == 0:
-                g[o] = work.tile([P, 4 * H * S], BF16, name="g", tag="g", bufs=1, align_bytes=64)
-            c0 = ((k % 2) * 2 + u) * H * S
+            if u == 0:
+                g[k] = work.tile([P, 2 * H * S], BF16, name="g", tag="g", bufs=1, align_bytes=64)
             nc.gpsimd.tensor_scalar(
-                out=g[o][:, c0:c0 + H * S].rearrange("p (h l t) -> p h l t", h=H, t=4),
+                out=g[k][:, u * H * S:(u + 1) * H * S].rearrange("p (h l t) -> p h l t", h=H, t=4),
                 in0=et_sb[m][:].rearrange("p (h t l) -> p h l t", h=H, t=4),
                 scalar1=1.0, scalar2=0.0, op0=ALU.mult, op1=ALU.add)
 
-        def st_w5(o):
-            codes[o] = work.tile([P, 8 * P], U32, name="codes", tag="codes", bufs=2, align_bytes=64)
-            scl[o] = work.tile([P, 8 * P], U8, name="scl", tag="scl", bufs=2, align_bytes=64)
-            nc.vector.quantize_mx(out=codes[o][:].bitcast(FP8X4), scales=scl[o][:], in_=g[o][:])
-            rinv[o] = work.tile([P, 8], F32, name="rinv", tag="rinv", bufs=3)
-            nc.vector.reciprocal(out=rinv[o][:], in_=rs[o][:])
+        def st_w5(k):
+            codes[k] = work.tile([P, 4 * P], U32, name="codes", tag="codes", bufs=2, align_bytes=64)
+            scl[k] = work.tile([P, 4 * P], U8, name="scl", tag="scl", bufs=2, align_bytes=64)
+            nc.vector.quantize_mx(out=codes[k][:].bitcast(FP8X4), scales=scl[k][:], in_=g[k][:])
+            rinv[k] = work.tile([P, 4], F32, name="rinv", tag="rinv", bufs=3)
+            nc.vector.reciprocal(out=rinv[k][:], in_=rs[k][:])
+
+        def st_w4p(k, u):
+            m = 2 * k + u
+            g_2[m] = work.tile([P, H * S], BF16, name="g_2", tag="g_2", bufs=4, align_bytes=64)
+            dst = g_2[m][:].rearrange("p (h l t) -> p h l t", h=H, t=4)
+            src = et[m][:].rearrange("p (h t l) -> p h l t", h=H, t=4)
+            if k == QUADS - 2:
+                nc.vector.tensor_copy(out=dst, in_=src)
+            else:
+                nc.scalar.copy(out=dst, in_=src)
+
+        def st_w5p(k, u):
+            m = 2 * k + u
+            codes[k, u] = work.tile([P, H * P], U32, name="codes_2", tag="codes_2", bufs=4, align_bytes=64)
+            scl[k, u] = work.tile([P, H * P], U8, name="scl_2", tag="scl_2", bufs=4, align_bytes=64)
+            nc.vector.quantize_mx(out=codes[k, u][:].bitcast(FP8X4), scales=scl[k, u][:], in_=g_2[m][:])
+            if u == 0:
+                rinv[k] = work.tile([P, 4], F32, name="rinv", tag="rinv", bufs=3)
+                nc.vector.reciprocal(out=rinv[k][:], in_=rs[k][:])
 
         def st_pv(k, u):
             m = 2 * k + u
             b = m // J
-            pv[m] = psum.tile([P, H * D], F32, name="pv", tag="pv", bufs=2)
-            o = k // 2
+            if k >= QUADS - 3:
+                pv[m] = psum.tile([P, H * D], F32, name="pv_late", tag="sc", bufs=3)
+            else:
+                pv[m] = psum.tile([P, H * D], F32, name="pv", tag="pv", bufs=2)
             for h in range(H):
-                i = (k % 2) * 4 + u * H + h
+                if direct(k):
+                    i = h
+                    words, plane = codes[k, u], scl[k, u]
+                else:
+                    i = u * H + h
+                    words, plane = codes[k], scl[k]
                 nc.tensor.matmul_mx(
                     out=pv[m][:, h * D:(h + 1) * D],
-                    lhsT=codes[o][:, i * P:(i + 1) * P].bitcast(FP8X4),
-                    lhsT_scale=scl[o][:, i * P:(i + 1) * P],
+                    lhsT=words[:, i * P:(i + 1) * P].bitcast(FP8X4),
+                    lhsT_scale=plane[:, i * P:(i + 1) * P],
                     rhs=v_codes[b][:, h * D:(h + 1) * D].bitcast(FP8X4),
                     rhs_scale=v_scales[b][:, h * D:(h + 1) * D],
                     start=True, stop=True)
@@ -311,13 +308,13 @@ def tile_dsattention_t_kernel(tc, queries, keys, values, tau, delta, out):
                 o_sb[k] = work.tile([P, 4 * D], F32, name="o_sb", tag="o_sb", bufs=3)
             for h in (1, 0):
                 i = u * H + h
-                r = rinv[k // 2][:, (k % 2) * 4 + i:(k % 2) * 4 + i + 1]
                 if w6_on_vector(k, u):
                     nc.vector.tensor_scalar_mul(
-                        out=o_sb[k][:, i * D:(i + 1) * D], in0=pv[m][:, h * D:(h + 1) * D], scalar1=r)
+                        out=o_sb[k][:, i * D:(i + 1) * D], in0=pv[m][:, h * D:(h + 1) * D], scalar1=rinv[k][:, i:i + 1])
                 else:
                     nc.scalar.activation(
-                        out=o_sb[k][:, i * D:(i + 1) * D], in_=pv[m][:, h * D:(h + 1) * D], func=ACT.Copy, scale=r)
+                        out=o_sb[k][:, i * D:(i + 1) * D], in_=pv[m][:, h * D:(h + 1) * D], func=ACT.Copy,
+                        scale=rinv[k][:, i:i + 1])
             if u == 1:
                 b, j = m // J, m % J
                 nc.sync.dma_start(
@@ -332,52 +329,45 @@ def tile_dsattention_t_kernel(tc, queries, keys, values, tau, delta, out):
         nc.scalar.copy(out=k_t[0][1][:], in_=kt1[:])
 
         for k in range(-1, QUADS + 4):
-            closes = ok(k - 3) and (k - 3) % 2 == 1
             if ok(k + 1) and k + 1 > 0:
                 st_w7(k + 1)
             if ok(k - 1):
                 st_w3(k - 1, 1, 0)
-                st_w3(k - 1, 1, 1)
-            if closes:
-                st_w5((k - 3) // 2)
-                st_pv(k - 4, 0)
-                st_pv(k - 4, 1)
+            if ok(k - 3) and not direct(k - 3):
+                st_w5(k - 3)
             elif k in (0, 1):
                 quantise_values(k)
-            if ok(k - 2):
+            if ok(k - 2) and direct(k - 2):
+                st_w5p(k - 2, 0)
+                st_w5p(k - 2, 1)
+            if ok(k - 2) and not direct(k - 2):
                 st_rg(k - 2, 0)
                 st_rg(k - 2, 1)
-            if ok(k - 4):
-                st_w6(k - 4, 0)
-            if ok(k - 1):
-                plan_et(k - 1, 0)
             if ok(k):
-                st_qk(k, 1, 1, False, 2)
+                st_qk(k, 1, 1)
+            if ok(k - 1):
+                st_et(k - 1, 0)
+            if ok(k):
                 st_w1(k, 0, 1)
+            if ok(k - 1):
+                st_w2(k - 1, 1, 1)
+                st_w3(k - 1, 1, 1)
             if ok(k + 1):
-                st_qk(k + 1, 0, 0, False, 2)
-            flush()
+                st_qk(k + 1, 0, 0)
             if ok(k):
                 st_w2(k, 0, 0)
                 st_w1(k, 1, 0)
+            if ok(k + 1):
+                st_qk(k + 1, 0, 1)
             if ok(k - 1):
-                plan_et_qt(k - 1, 1, k + 2)
-            elif ok(k + 2):
+                st_et(k - 1, 1)
+            if ok(k + 2):
                 st_qt(k + 2)
-            if ok(k + 1):
-                st_qk(k + 1, 0, 1, False, 3)
-            if ok(k):
-                st_w2(k, 0, 1)
-            if ok(k - 4) and w6_on_vector(k - 4, 1):
-                st_w6(k - 4, 1)
-            if ok(k):
-                st_w1(k, 1, 1)
-            if ok(k + 1):
-                st_qk(k + 1, 1, 0, True, 3)
-            flush()
             if ok(k):
                 st_w3(k, 0, 0)
-            if ok(k - 1):
+            if ok(k - 4):
+                st_w6(k - 4, 0)
+            if ok(k - 1) and not direct(k - 1):
                 st_w4(k - 1, 0)
             elif k == 0:
                 kt0 = prepare_keys(1, 0, "pv", 2)
@@ -385,18 +375,24 @@ def tile_dsattention_t_kernel(tc, queries, keys, values, tau, delta, out):
             if k == 1:
                 kt0 = spread_delta(0)
                 nc.scalar.copy(out=d_t[:, 0:S], in_=kt0[:])
-            if ok(k - 4) and not w6_on_vector(k - 4, 1):
+            if ok(k):
+                st_w2(k, 0, 1)
+            if ok(k - 4):
                 st_w6(k - 4, 1)
-            if closes:
+            if ok(k):
+                st_w1(k, 1, 1)
+            if ok(k + 1):
+                st_qk(k + 1, 1, 0)
+            if ok(k - 3):
                 st_pv(k - 3, 0)
                 st_pv(k - 3, 1)
+            if ok(k):
+                st_w2(k, 1, 0)
             if ok(k + 1):
                 st_w1(k + 1, 0, 0)
             if ok(k):
-                st_w2(k, 1, 0)
-                st_w2(k, 1, 1)
                 st_w3(k, 0, 1)
-            if ok(k - 1):
+            if ok(k - 1) and not direct(k - 1):
                 st_w4(k - 1, 1)
             elif k == 0:
                 kt1 = prepare_keys(1, 1, "pv", 2)
@@ -404,3 +400,6 @@ def tile_dsattention_t_kernel(tc, queries, keys, values, tau, delta, out):
             if k == 1:
                 kt1 = spread_delta(1)
                 nc.scalar.copy(out=d_t[:, S:2 * S], in_=kt1[:])
+            if ok(k - 1) and direct(k - 1):
+                st_w4p(k - 1, 0)
+                st_w4p(k - 1, 1)

@@ -141,13 +141,13 @@ def tile_dsattention_t_kernel(tc, queries, keys, values, tau, delta, out):
             return u == 1 and h == 1 and 3 <= k < 28
 
         def by_transpose(k, u, h):
-            return h == 1 and k >= 3 and ((u == 1 and k >= 28) or (u == 0 and k % 2 == 1))
+            return h == 1 and k >= 3 and ((u == 1 and k >= 28) or (u == 0 and k % 4 != 0))
 
         def on_pe(k, u, h):
             return by_matmul(k, u, h) or by_transpose(k, u, h)
 
         def w6_on_vector(k, u):
-            return u == 1 and (k % 3 != 2 or k >= QUADS - 4)
+            return u == 1
 
         def direct(k):
             return k >= QUADS - 2
@@ -242,16 +242,15 @@ def tile_dsattention_t_kernel(tc, queries, keys, values, tau, delta, out):
 
         def st_w4(k, u):
             m = 2 * k + u
-            et_sb[m] = work.tile([P, H * S], BF16, name="et_sb", tag="et_sb", bufs=3)
-            nc.scalar.copy(out=et_sb[m][:], in_=et[m][:])
-
-        def st_rg(k, u):
-            m = 2 * k + u
             if u == 0:
-                g[k] = work.tile([P, 2 * H * S], BF16, name="g", tag="g", bufs=1, align_bytes=64)
+                et_sb[k] = work.tile([P, 2 * H * S], BF16, name="et_sb", tag="et_sb", bufs=3)
+            nc.scalar.copy(out=et_sb[k][:, u * H * S:(u + 1) * H * S], in_=et[m][:])
+
+        def st_rg(k):
+            g[k] = work.tile([P, 2 * H * S], BF16, name="g", tag="g", bufs=1, align_bytes=64)
             nc.gpsimd.tensor_scalar(
-                out=g[k][:, u * H * S:(u + 1) * H * S].rearrange("p (h l t) -> p h l t", h=H, t=4),
-                in0=et_sb[m][:].rearrange("p (h t l) -> p h l t", h=H, t=4),
+                out=g[k][:].rearrange("p (i l t) -> p i l t", i=4, t=4),
+                in0=et_sb[k][:].rearrange("p (i t l) -> p i l t", i=4, t=4),
                 scalar1=1.0, scalar2=0.0, op0=ALU.mult, op1=ALU.add)
 
         def st_w5(k):
@@ -341,8 +340,7 @@ def tile_dsattention_t_kernel(tc, queries, keys, values, tau, delta, out):
                 st_w5p(k - 2, 0)
                 st_w5p(k - 2, 1)
             if ok(k - 2) and not direct(k - 2):
-                st_rg(k - 2, 0)
-                st_rg(k - 2, 1)
+                st_rg(k - 2)
             if ok(k):
                 st_qk(k, 1, 1)
             if ok(k - 1):

from contextlib import ExitStack

import concourse.bass as bass
import concourse.masks as masks
import concourse.mybir as mybir
import concourse.tile as tile

F32 = mybir.dt.float32
BF16 = mybir.dt.bfloat16
U32 = mybir.dt.uint32
U8 = mybir.dt.uint8
FP8X4 = mybir.dt.float8_e4m3fn_x4
ALU = mybir.AluOpType
ACT = mybir.ActivationFunctionType
AX = mybir.AxisListType

B, L, S, H, D = 2, 4096, 512, 2, 256
P = 128
J = L // P
PAIRS = B * J
QUADS = PAIRS // 2
QCH = 8
FLOPS = 2 * 2 * B * H * L * S * D
MANUAL = True


def tile_dsattention_t_kernel(tc, queries, keys, values, tau, delta, out):
    nc = tc.nc
    with ExitStack() as ctx:
        const = ctx.enter_context(tc.tile_pool(name="const", bufs=1))
        work = ctx.enter_context(tc.tile_pool(name="work", bufs=3))
        psum = ctx.enter_context(tc.psum_pool(name="psum", bufs=1))
        if MANUAL:
            ctx.enter_context(tc.manual_schedule())

        k_raw = [const.tile([P, 4 * H * D], BF16, name="k_raw%d" % b) for b in range(B)]
        v_raw = [const.tile([P, 4 * H * D], BF16, name="v_raw%d" % b) for b in range(B)]
        q_sb = [const.tile([P, J * H * D], BF16, name="q_sb%d" % b) for b in range(B)]
        tau_bf = const.tile([P, B], BF16, name="tau_bf")
        delta_bf = const.tile([P, B * S], BF16, name="delta_bf")

        def load_kv(dst, src, b):
            nc.sync.dma_start(
                out=dst[b][:].rearrange("p (t c) -> p t c", t=4),
                in_=src[b].rearrange("(t p) h d -> p t (h d)", p=P),
            )

        def load_q(b, j0, j1):
            nc.sync.dma_start(
                out=q_sb[b][:].rearrange("p (j c) -> p j c", j=J)[:, j0:j1, :],
                in_=queries[b].rearrange("(p j) h d -> p j (h d)", j=J)[:, j0:j1, :],
            )

        load_kv(k_raw, keys, 0)
        load_q(0, 0, 2)
        nc.sync.dma_start(out=tau_bf[:], in_=tau.partition_broadcast(P))
        nc.sync.dma_start(out=delta_bf[:], in_=delta.rearrange("b s -> (b s)").partition_broadcast(P))
        load_q(0, 2, QCH)
        load_kv(v_raw, values, 0)
        load_kv(k_raw, keys, 1)
        load_kv(v_raw, values, 1)
        for c in range(1, J // QCH):
            load_q(0, c * QCH, (c + 1) * QCH)
        for c in range(J // QCH):
            load_q(1, c * QCH, (c + 1) * QCH)

        ident_f = const.tile([P, P], F32, name="ident_f")
        masks.make_identity(nc, ident_f[:])
        ident_b = const.tile([P, P], BF16, name="ident_b")
        masks.make_identity(nc, ident_b[:])
        ntau = const.tile([P, B], F32, name="ntau")
        nc.gpsimd.tensor_scalar(out=ntau[:], in0=tau_bf[:], scalar1=-1.0 / 16.0, scalar2=0.0, op0=ALU.mult, op1=ALU.add)
        ndelta = const.tile([P, B * S], F32, name="ndelta")
        nc.gpsimd.tensor_scalar(out=ndelta[:], in0=delta_bf[:], scalar1=-1.0 / 16.0, scalar2=0.0, op0=ALU.mult, op1=ALU.add)

        k_t = [[const.tile([P, S], F32, name="k_t%d%d" % (b, h)) for h in range(H)] for b in range(B)]
        v_codes = [const.tile([P, H * D], U32, name="v_codes%d" % b, align_bytes=64) for b in range(B)]
        v_scales = [const.tile([P, H * D], U8, name="v_scales%d" % b, align_bytes=64) for b in range(B)]

        def prepare_keys(b, h, tag, bufs):
            words = k_raw[b][:].bitcast(F32)
            kt_ps = psum.tile([P, S], F32, name="kt_ps", tag=tag, bufs=bufs)
            for t in range(4):
                c0 = t * (H * D // 2) + h * (D // 2)
                nc.tensor.transpose(kt_ps[:, t * P:(t + 1) * P], words[:, c0:c0 + P], ident_f[:])
            return kt_ps

        def regroup_values(b):
            v_grp = const.tile([P, 4 * H * D], BF16, name="v_grp%d" % b, align_bytes=64)
            nc.gpsimd.tensor_scalar(
                out=v_grp[:].rearrange("p (c t) -> p c t", t=4),
                in0=v_raw[b][:].rearrange("p (t c) -> p c t", t=4),
                scalar1=1.0, scalar2=0.0, op0=ALU.mult, op1=ALU.add)
            return v_grp

        def quantise_values(b):
            nc.vector.quantize_mx(out=v_codes[b][:].bitcast(FP8X4), scales=v_scales[b][:], in_=grp[b][:])

        grp = [regroup_values(b) for b in range(B)]

        ones_bf = const.tile([P, P], BF16, name="ones_bf")
        nc.gpsimd.memset(ones_bf[:], 1.0)
        itau = const.tile([P, B], F32, name="itau")
        hi_b = const.tile([P, B], BF16, name="hi_b")
        mid_b = const.tile([P, B], BF16, name="mid_b")
        lo_b = const.tile([P, B], BF16, name="lo_b")
        r_1 = const.tile([P, B], F32, name="r_1")
        r_2 = const.tile([P, B], F32, name="r_2")
        c_0 = const.tile([P, B], F32, name="c_0")
        c_1 = const.tile([P, B], F32, name="c_1")
        c_2 = const.tile([P, B], F32, name="c_2")
        w_d = [const.tile([P, P], BF16, name="w_d%d" % b) for b in range(B)]
        dtau = const.tile([P, B * S], F32, name="dtau")
        d_t = const.tile([P, B * S], F32, name="d_t")
        small = [
            lambda: nc.vector.reciprocal(out=itau[:], in_=tau_bf[:]),
            lambda: nc.vector.tensor_scalar_mul(out=dtau[:, 0:S], in0=delta_bf[:, 0:S], scalar1=itau[:, 0:1]),
            lambda: nc.vector.tensor_scalar_mul(out=dtau[:, S:2 * S], in0=delta_bf[:, S:2 * S], scalar1=itau[:, 1:2]),
            lambda: nc.vector.tensor_copy(out=hi_b[:], in_=itau[:]),
            lambda: nc.vector.tensor_tensor(out=r_1[:], in0=itau[:], in1=hi_b[:], op=ALU.subtract),
            lambda: nc.vector.tensor_copy(out=mid_b[:], in_=r_1[:]),
            lambda: nc.vector.tensor_tensor(out=r_2[:], in0=r_1[:], in1=mid_b[:], op=ALU.subtract),
            lambda: nc.vector.tensor_copy(out=lo_b[:], in_=r_2[:]),
            lambda: nc.vector.tensor_scalar_mul(out=c_0[:], in0=hi_b[:], scalar1=ident_f[:, 0:1]),
            lambda: nc.vector.scalar_tensor_tensor(
                out=c_1[:], in0=mid_b[:], scalar=ident_f[:, 1:2], in1=c_0[:], op0=ALU.mult, op1=ALU.add),
            lambda: nc.vector.scalar_tensor_tensor(
                out=c_2[:], in0=lo_b[:], scalar=ident_f[:, 2:3], in1=c_1[:], op0=ALU.mult, op1=ALU.add),
            lambda: nc.vector.tensor_scalar_mul(out=w_d[0][:], in0=ones_bf[:], scalar1=c_2[:, 0:1]),
            lambda: nc.vector.tensor_scalar_mul(out=w_d[1][:], in0=ones_bf[:], scalar1=c_2[:, 1:2]),
        ]

        done_small = [0]

        def one_small():
            if done_small[0] < len(small):
                small[done_small[0]]()
                done_small[0] += 1

        def by_matmul(k, u, h):
            return u == 1 and h == 1 and 3 <= k < 28

        def by_transpose(k, u, h):
            return h == 1 and k >= 3 and ((u == 1 and k >= 28) or (u == 0 and k % 4 != 0))

        def on_pe(k, u, h):
            return by_matmul(k, u, h) or by_transpose(k, u, h)

        def w6_on_vector(k, u):
            return u == 1

        def direct(k):
            return k >= QUADS - 2

        def spread_delta(b):
            dt_ps = psum.tile([P, S], F32, name="dt_ps", tag="pv", bufs=2)
            for t in range(4):
                c0 = b * S + t * P
                nc.tensor.transpose(dt_ps[:, t * P:(t + 1) * P], dtau[:, c0:c0 + P], ident_f[:])
            return dt_ps

        qt_ps, q_t, sc, nz, mn, rs, e_sb, et, et_sb, g, codes, scl, rinv, pv, o_sb, g_2 = (
            {}, {}, {}, {}, {}, {}, {}, {}, {}, {}, {}, {}, {}, {}, {}, {})

        def ok(k):
            return 0 <= k < QUADS

        def st_qt(k):
            qt_ps[k] = psum.tile([P, 4 * P], F32, name="qt_ps", tag="qt", bufs=1)
            for u in range(2):
                m = 2 * k + u
                words = q_sb[m // J][:].bitcast(F32)
                for h in range(H):
                    c0 = (m % J) * (H * D // 2) + h * (D // 2)
                    i = u * H + h
                    nc.tensor.transpose(qt_ps[k][:, i * P:(i + 1) * P], words[:, c0:c0 + P], ident_f[:])

        def st_w7(k):
            q_t[k] = work.tile([P, 4 * P], F32, name="q_t", tag="q_t", bufs=3)
            if k == 0:
                nc.vector.tensor_copy(out=q_t[k][:], in_=qt_ps[k][:])
            else:
                nc.scalar.copy(out=q_t[k][:], in_=qt_ps[k][:])

        def st_qk(k, u, h):
            m = 2 * k + u
            b = m // J
            sc[m, h] = psum.tile([P, S], F32, name="sc", tag="sc", bufs=3)
            qv = q_t[k][:].bitcast(BF16).rearrange("p (i l e) -> p i l e", i=4, e=2)
            kv = k_t[b][h][:].bitcast(BF16).rearrange("p (s e) -> p s e", e=2)
            for e in range(2):
                nc.tensor.matmul(
                    sc[m, h][:], lhsT=qv[:, u * H + h, :, e], rhs=kv[:, :, e], start=(e == 0),
                    stop=(e == 1 and not on_pe(k, u, h)))
            if by_matmul(k, u, h):
                nc.tensor.matmul(sc[m, h][:], lhsT=w_d[b][:], rhs=delta_bf[:, b * S:(b + 1) * S], start=False, stop=True)
            if by_transpose(k, u, h):
                for t in range(4):
                    c0 = b * S + t * P
                    nc.tensor.matmul(
                        sc[m, h][:, t * P:(t + 1) * P], lhsT=d_t[:, c0:c0 + P], rhs=ident_f[:], is_transpose=True,
                        start=False, stop=(t == 3))

        def st_w1(k, u, h):
            m = 2 * k + u
            b = m // J
            nz[m, h] = work.tile([P, S], F32, name="nz", tag="nz", bufs=10)
            if on_pe(k, u, h):
                mn[m, h] = work.tile([P, 1], F32, name="mn", tag="mn", bufs=12)
                nc.vector.tensor_scalar(
                    out=nz[m, h][:], in0=sc[m, h][:], scalar1=ntau[:, b:b + 1], scalar2=None,
                    op0=ALU.mult, op1=ALU.min, accum_out=mn[m, h][:])
            else:
                nc.vector.scalar_tensor_tensor(
                    out=nz[m, h][:], in0=sc[m, h][:], scalar=ntau[:, b:b + 1],
                    in1=ndelta[:, b * S:(b + 1) * S], op0=ALU.mult, op1=ALU.add)
            one_small()

        def st_w2(k, u, h):
            m = 2 * k + u
            if on_pe(k, u, h):
                return
            mn[m, h] = work.tile([P, 1], F32, name="mn", tag="mn", bufs=12)
            nc.vector.tensor_reduce(out=mn[m, h][:], in_=nz[m, h][:], axis=AX.X, op=ALU.min)

        def st_w3(k, u, h):
            m = 2 * k + u
            if u == 0 and h == 0:
                rs[k] = work.tile([P, 4], F32, name="rs", tag="rs", bufs=5)
            if m not in e_sb:
                e_sb[m] = work.tile([P, H * S], BF16, name="e_sb", tag="e_sb", bufs=4)
            i = u * H + h
            nc.scalar.activation(
                out=e_sb[m][:, h * S:(h + 1) * S], in_=nz[m, h][:], func=ACT.Exp, bias=mn[m, h][:], scale=-1.0,
                accum_out=rs[k][:, i:i + 1])

        def st_et(k, u):
            m = 2 * k + u
            et[m] = psum.tile([P, H * S], BF16, name="et", tag="et", bufs=2)
            for i in range(8):
                nc.tensor.transpose(et[m][:, i * P:(i + 1) * P], e_sb[m][:, i * P:(i + 1) * P], ident_b[:])

        def st_w4(k, u):
            m = 2 * k + u
            if u == 0:
                et_sb[k] = work.tile([P, 2 * H * S], BF16, name="et_sb", tag="et_sb", bufs=3)
            nc.scalar.copy(out=et_sb[k][:, u * H * S:(u + 1) * H * S], in_=et[m][:])

        def st_rg(k):
            g[k] = work.tile([P, 2 * H * S], BF16, name="g", tag="g", bufs=1, align_bytes=64)
            nc.gpsimd.tensor_scalar(
                out=g[k][:].rearrange("p (i l t) -> p i l t", i=4, t=4),
                in0=et_sb[k][:].rearrange("p (i t l) -> p i l t", i=4, t=4),
                scalar1=1.0, scalar2=0.0, op0=ALU.mult, op1=ALU.add)

        def st_w5(k):
            codes[k] = work.tile([P, 4 * P], U32, name="codes", tag="codes", bufs=2, align_bytes=64)
            scl[k] = work.tile([P, 4 * P], U8, name="scl", tag="scl", bufs=2, align_bytes=64)
            nc.vector.quantize_mx(out=codes[k][:].bitcast(FP8X4), scales=scl[k][:], in_=g[k][:])
            rinv[k] = work.tile([P, 4], F32, name="rinv", tag="rinv", bufs=3)
            nc.vector.reciprocal(out=rinv[k][:], in_=rs[k][:])

        def st_w4p(k, u):
            m = 2 * k + u
            g_2[m] = work.tile([P, H * S], BF16, name="g_2", tag="g_2", bufs=4, align_bytes=64)
            dst = g_2[m][:].rearrange("p (h l t) -> p h l t", h=H, t=4)
            src = et[m][:].rearrange("p (h t l) -> p h l t", h=H, t=4)
            if k == QUADS - 2:
                nc.vector.tensor_copy(out=dst, in_=src)
            else:
                nc.scalar.copy(out=dst, in_=src)

        def st_w5p(k, u):
            m = 2 * k + u
            codes[k, u] = work.tile([P, H * P], U32, name="codes_2", tag="codes_2", bufs=4, align_bytes=64)
            scl[k, u] = work.tile([P, H * P], U8, name="scl_2", tag="scl_2", bufs=4, align_bytes=64)
            nc.vector.quantize_mx(out=codes[k, u][:].bitcast(FP8X4), scales=scl[k, u][:], in_=g_2[m][:])
            if u == 0:
                rinv[k] = work.tile([P, 4], F32, name="rinv", tag="rinv", bufs=3)
                nc.vector.reciprocal(out=rinv[k][:], in_=rs[k][:])

        def st_pv(k, u):
            m = 2 * k + u
            b = m // J
            if k >= QUADS - 3:
                pv[m] = psum.tile([P, H * D], F32, name="pv_late", tag="sc", bufs=3)
            else:
                pv[m] = psum.tile([P, H * D], F32, name="pv", tag="pv", bufs=2)
            for h in range(H):
                if direct(k):
                    i = h
                    words, plane = codes[k, u], scl[k, u]
                else:
                    i = u * H + h
                    words, plane = codes[k], scl[k]
                nc.tensor.matmul_mx(
                    out=pv[m][:, h * D:(h + 1) * D],
                    lhsT=words[:, i * P:(i + 1) * P].bitcast(FP8X4),
                    lhsT_scale=plane[:, i * P:(i + 1) * P],
                    rhs=v_codes[b][:, h * D:(h + 1) * D].bitcast(FP8X4),
                    rhs_scale=v_scales[b][:, h * D:(h + 1) * D],
                    start=True, stop=True)

        def st_w6(k, u):
            m = 2 * k + u
            if u == 0:
                o_sb[k] = work.tile([P, 4 * D], F32, name="o_sb", tag="o_sb", bufs=3)
            for h in (1, 0):
                i = u * H + h
                if w6_on_vector(k, u):
                    nc.vector.tensor_scalar_mul(
                        out=o_sb[k][:, i * D:(i + 1) * D], in0=pv[m][:, h * D:(h + 1) * D], scalar1=rinv[k][:, i:i + 1])
                else:
                    nc.scalar.activation(
                        out=o_sb[k][:, i * D:(i + 1) * D], in_=pv[m][:, h * D:(h + 1) * D], func=ACT.Copy,
                        scale=rinv[k][:, i:i + 1])
            if u == 1:
                b, j = m // J, m % J
                nc.sync.dma_start(
                    out=out[b].rearrange("(p j) h d -> p j (h d)", j=J)[:, j - 1:j + 1, :],
                    in_=o_sb[k][:].rearrange("p (j c) -> p j c", j=2))

        kt0 = prepare_keys(0, 0, "sc", 3)
        st_qt(0)
        nc.scalar.copy(out=k_t[0][0][:], in_=kt0[:])
        kt1 = prepare_keys(0, 1, "sc", 3)
        st_w7(0)
        nc.scalar.copy(out=k_t[0][1][:], in_=kt1[:])

        for k in range(-1, QUADS + 4):
            if ok(k + 1) and k + 1 > 0:
                st_w7(k + 1)
            if ok(k - 1):
                st_w3(k - 1, 1, 0)
            if ok(k - 3) and not direct(k - 3):
                st_w5(k - 3)
            elif k in (0, 1):
                quantise_values(k)
            if ok(k - 2) and direct(k - 2):
                st_w5p(k - 2, 0)
                st_w5p(k - 2, 1)
            if ok(k - 2) and not direct(k - 2):
                st_rg(k - 2)
            if ok(k):
                st_qk(k, 1, 1)
            if ok(k - 1):
                st_et(k - 1, 0)
            if ok(k):
                st_w1(k, 0, 1)
            if ok(k - 1):
                st_w2(k - 1, 1, 1)
                st_w3(k - 1, 1, 1)
            if ok(k + 1):
                st_qk(k + 1, 0, 0)
            if ok(k):
                st_w2(k, 0, 0)
                st_w1(k, 1, 0)
            if ok(k + 1):
                st_qk(k + 1, 0, 1)
            if ok(k - 1):
                st_et(k - 1, 1)
            if ok(k + 2):
                st_qt(k + 2)
            if ok(k):
                st_w3(k, 0, 0)
            if ok(k - 4):
                st_w6(k - 4, 0)
            if ok(k - 1) and not direct(k - 1):
                st_w4(k - 1, 0)
            elif k == 0:
                kt0 = prepare_keys(1, 0, "pv", 2)
                nc.scalar.copy(out=k_t[1][0][:], in_=kt0[:])
            if k == 1:
                kt0 = spread_delta(0)
                nc.scalar.copy(out=d_t[:, 0:S], in_=kt0[:])
            if ok(k):
                st_w2(k, 0, 1)
            if ok(k - 4):
                st_w6(k - 4, 1)
            if ok(k):
                st_w1(k, 1, 1)
            if ok(k + 1):
                st_qk(k + 1, 1, 0)
            if ok(k - 3):
                st_pv(k - 3, 0)
                st_pv(k - 3, 1)
            if ok(k):
                st_w2(k, 1, 0)
            if ok(k + 1):
                st_w1(k + 1, 0, 0)
            if ok(k):
                st_w3(k, 0, 1)
            if ok(k - 1) and not direct(k - 1):
                st_w4(k - 1, 1)
            elif k == 0:
                kt1 = prepare_keys(1, 1, "pv", 2)
                nc.scalar.copy(out=k_t[1][1][:], in_=kt1[:])
            if k == 1:
                kt1 = spread_delta(1)
                nc.scalar.copy(out=d_t[:, S:2 * S], in_=kt1[:])
            if ok(k - 1) and direct(k - 1):
                st_w4p(k - 1, 0)
                st_w4p(k - 1, 1)
